import numpy as np
import ml_dtypes


def mxq(x, axis, fmt="e4m3"):
    dtype, down = {"e4m3": (ml_dtypes.float8_e4m3fn, 7), "e5m2": (ml_dtypes.float8_e5m2, 14)}[fmt]
    v = np.moveaxis(np.asarray(x, np.float32).astype(ml_dtypes.bfloat16).astype(np.float64), axis, -1)
    blocks = v.reshape(v.shape[:-1] + (-1, 32))
    amax = np.abs(blocks).max(-1, keepdims=True)
    byte = np.maximum(np.where(amax > 0, np.frexp(amax)[1] - 1 + 127, 0) - down, 1)
    scale = np.exp2(byte - 127.0)
    codes = (blocks / scale).astype(np.float32).astype(dtype).astype(np.float64)
    return np.moveaxis((codes * scale).reshape(v.shape), -1, axis)


WIDE = False


def mx_kscale(k):
    if not WIDE:
        return np.ones(k)
    levels = np.array([10, -10, 5, -5, 0])
    a = np.random.permutation(np.resize(levels, k // 512 * 4)).reshape(k // 512, 4)
    idx = np.arange(k)
    return np.exp2(a[idx // 512, idx % 128 // 32])


BF16 = ml_dtypes.bfloat16


def bf(x):
    return np.asarray(x, np.float32).astype(BF16)


def f64(x):
    return np.asarray(x).astype(np.float64)


E2M1 = np.array([0.0, 0.5, 1.0, 1.5, 2.0, 3.0, 4.0, 6.0, -0.0, -0.5, -1.0, -1.5, -2.0, -3.0, -4.0, -6.0])


def pack_weight(w, fmt):
    k, n = w.shape
    w = f64(bf(w)).reshape(k // 32, 32, n)
    amax = np.abs(w).max(1)
    if fmt == "e4m3":
        byte = np.frexp(amax)[1] - 1 + 127 - 7
    else:
        mant, ex = np.frexp(amax / 6.0)
        byte = np.where(mant > 0.5, ex, ex - 1) + 127
    byte = np.clip(np.where(amax > 0, byte, 1), 1, 254)
    scaled = (w * np.exp2(127.0 - byte)[:, None, :]).reshape(k, n).astype(np.float32)
    by_word = np.ascontiguousarray(scaled.reshape(k // 512, 128, 4, n).transpose(0, 1, 3, 2))
    if fmt == "e4m3":
        words = by_word.astype(ml_dtypes.float8_e4m3fn).view(np.uint8)
    else:
        c = by_word.astype(ml_dtypes.float4_e2m1fn).view(np.uint8) & 0xF
        words = c[..., 0::2] | (c[..., 1::2] << 4)
    return np.ascontiguousarray(words), np.ascontiguousarray(byte.astype(np.uint8).reshape(k // 512, 16, n))


def unpack_weight(words, scales, fmt):
    g, p, n, _ = words.shape
    if fmt == "e4m3":
        vals = np.ascontiguousarray(words).view(ml_dtypes.float8_e4m3fn).astype(np.float64)
    else:
        nib = np.empty((g, p, n, 4), np.uint8)
        nib[..., 0::2] = words & 0xF
        nib[..., 1::2] = words >> 4
        vals = E2M1[nib]
    vals = vals * np.repeat(np.exp2(scales.astype(np.float64) - 127.0), 8, axis=1)[..., None]
    return vals.transpose(0, 1, 3, 2).reshape(g * 512, n)


B, I, H = 512, 512, 2048
K = I + H
FMT = "e4m3"


def setup_inputs():
    s = mx_kscale(I)
    sk = np.concatenate([s, np.ones(H)])
    x = bf(np.random.standard_normal((B, I)) * s)
    h = bf(np.random.standard_normal((B, H)))
    time_delta = bf(np.random.uniform(0.0, 1.0, (B, 1)))
    W_mod_words, W_mod_scales = pack_weight(np.random.standard_normal((K, H)) * 0.6 / np.sqrt(K) / sk[:, None], FMT)
    b_mod = bf(np.random.standard_normal(H) * 0.2)
    W_tgt_words, W_tgt_scales = pack_weight(np.random.standard_normal((K, H)) * 0.6 / np.sqrt(K) / sk[:, None], FMT)
    b_tgt = bf(np.random.standard_normal(H) * 0.2)
    log_tau = bf(np.random.standard_normal(H) * 0.2)
    bias = bf(np.random.standard_normal(H) * 0.1)
    return {"x": x,
            "h": h,
            "time_delta": time_delta,
            "W_mod_words": W_mod_words,
            "W_mod_scales": W_mod_scales,
            "b_mod": b_mod,
            "W_tgt_words": W_tgt_words,
            "W_tgt_scales": W_tgt_scales,
            "b_tgt": b_tgt,
            "log_tau": log_tau,
            "bias": bias}


def reference(x, h, time_delta, W_mod_words, W_mod_scales, b_mod, W_tgt_words, W_tgt_scales, b_tgt, log_tau, bias):
    hf = f64(h)
    combined = np.concatenate([f64(x), hf], axis=-1)
    cq = mxq(combined, 1, "e4m3")
    f = np.tanh((cq @ unpack_weight(W_mod_words, W_mod_scales, FMT)) + f64(b_mod))
    a = np.tanh((cq @ unpack_weight(W_tgt_words, W_tgt_scales, FMT)) + f64(b_tgt))
    tau = np.exp(f64(log_tau))[None, :]
    tau_sys = tau / (1.0 + tau * np.abs(f))
    decay = np.exp(-f64(time_delta) / (tau_sys + 1e-6))
    h_new = decay * hf + (1.0 - decay) * (a + f64(bias))
    return h_new

@@ -1,0 +1,261 @@
+from contextlib import ExitStack
+
+import concourse.mybir as mybir
+from concourse.masks import make_identity
+
+F32 = mybir.dt.float32
+BF16 = mybir.dt.bfloat16
+I32 = mybir.dt.int32
+U32 = mybir.dt.uint32
+U8 = mybir.dt.uint8
+FP8X4 = mybir.dt.float8_e4m3fn_x4
+ACT = mybir.ActivationFunctionType
+ALU = mybir.AluOpType
+
+P = 128
+PACK = 4
+K_PASS = P * PACK
+BATCH = 512
+IN = 512
+HID = 2048
+K = IN + HID
+PASSES = K // K_PASS
+B_TILES = BATCH // P
+ROUND_TILES = 2
+ROUND_COLS = ROUND_TILES * P
+ROUNDS = HID // ROUND_COLS
+PLANES_PER_TILE = 4
+EPS = 1e-6
+
+FLOPS = 2 * 2 * BATCH * K * HID
+
+
+def tile_ltccell_kernel(
+    tc, x, h, time_delta, W_mod_words, W_mod_scales, b_mod, W_tgt_words, W_tgt_scales, b_tgt, log_tau, bias, out
+):
+    nc = tc.nc
+    with ExitStack() as ctx:
+        keep = ctx.enter_context(tc.tile_pool(name="keep", bufs=1))
+        stage = ctx.enter_context(tc.tile_pool(name="stage", bufs=2))
+        work = ctx.enter_context(tc.tile_pool(name="work", bufs=2))
+        mx_psum = ctx.enter_context(tc.psum_pool(name="mx_psum", bufs=4))
+        flip_psum = ctx.enter_context(tc.psum_pool(name="flip_psum", bufs=4))
+        ctx.enter_context(tc.manual_schedule())
+
+
+        planes_mod = keep.tile([P, HID], U8, align_bytes=64)
+        planes_tgt = keep.tile([P, HID], U8, align_bytes=64)
+        planes_last = keep.tile([P, HID], U8, align_bytes=64)
+        for plane in (planes_mod, planes_tgt, planes_last):
+            nc.vector.memset(plane[:].bitcast(I32), 0)
+
+        n_tiles = HID // P
+        vec_rows = keep.tile([P, P], BF16)
+        nc.vector.memset(vec_rows[:], 0.0)
+        first_row = {}
+        for position, (name, vec) in enumerate(
+            (("b_mod", b_mod), ("b_tgt", b_tgt), ("log_tau", log_tau), ("bias", bias))
+        ):
+            first_row[name] = n_tiles * position
+            nc.scalar.dma_start(
+                out=vec_rows[n_tiles * position : n_tiles * (position + 1), :],
+                in_=vec.rearrange("(r c) -> r c", c=P),
+            )
+        first_row["dt"] = 4 * n_tiles
+        nc.scalar.dma_start(
+            out=vec_rows[4 * n_tiles : 4 * n_tiles + B_TILES, :], in_=time_delta.rearrange("(r c) o -> r (c o)", c=P)
+        )
+
+        c_sb = keep.tile([P, B_TILES, K], BF16)
+        x_view = x.rearrange("(j p) k -> p j k", p=P)
+        h_view = h.rearrange("(j p) k -> p j k", p=P)
+        nc.gpsimd.dma_start(out=c_sb[:, :, 0:IN], in_=x_view)
+        ident_f32 = keep.tile([P, P], F32)
+        make_identity(nc, ident_f32[:])
+        ident_bf16 = keep.tile([P, P], BF16)
+        nc.vector.tensor_copy(out=ident_bf16[:], in_=ident_f32[:])
+        for g in range(1, PASSES):
+            nc.gpsimd.dma_start(
+                out=c_sb[:, :, K_PASS * g : K_PASS * (g + 1)], in_=h_view[:, :, K_PASS * (g - 1) : K_PASS * g]
+            )
+
+        for w, (scales, plane) in enumerate(((W_mod_scales, planes_mod), (W_tgt_scales, planes_tgt))):
+            for quad in range(4):
+                rows = slice(4 * quad, 4 * quad + 4)
+                nc.sync.dma_start(
+                    out=plane[32 * quad : 32 * quad + 16, :].bitcast(I32),
+                    in_=scales[0:PLANES_PER_TILE, rows, :].bitcast(I32),
+                )
+                nc.sync.dma_start(
+                    out=planes_last[32 * quad + 4 * w : 32 * quad + 4 * w + 4, :].bitcast(I32),
+                    in_=scales[PLANES_PER_TILE, rows, :].bitcast(I32),
+                )
+
+        w_mod_sb = keep.tile([P, PASSES, HID], U32, align_bytes=64)
+        w_tgt_sb = keep.tile([P, PASSES, HID], U32, align_bytes=64)
+        for r in range(ROUNDS):
+            for words, w_sb in ((W_mod_words, w_mod_sb), (W_tgt_words, w_tgt_sb)):
+                nc.sync.dma_start(
+                    out=w_sb[:, :, ROUND_COLS * r : ROUND_COLS * (r + 1)].bitcast(I32),
+                    in_=words.rearrange("g p n t -> p g (n t)")[
+                        :, :, PACK * ROUND_COLS * r : PACK * ROUND_COLS * (r + 1)
+                    ].bitcast(I32),
+                )
+
+        vec_ps = flip_psum.tile([P, P], BF16, tag="flip")
+        nc.tensor.transpose(vec_ps[:], vec_rows[:], ident_bf16[:])
+        vec_cols = keep.tile([P, P], F32)
+        nc.vector.tensor_copy(out=vec_cols[:], in_=vec_ps[:])
+
+        def columns(name, count):
+            return vec_cols[:, first_row[name] : first_row[name] + count]
+
+        inv_tau = keep.tile([P, n_tiles], F32)
+        seed = keep.tile([P, n_tiles], F32)
+        slope = keep.tile([P, n_tiles], F32)
+        neg_dt = keep.tile([P, B_TILES], F32)
+        nc.scalar.activation(out=inv_tau[:], in_=columns("log_tau", n_tiles), func=ACT.Exp, scale=-1.0)
+        nc.vector.tensor_scalar(out=seed[:], in0=inv_tau[:], scalar1=EPS, scalar2=1.0, op0=ALU.mult, op1=ALU.add)
+        nc.vector.reciprocal(out=seed[:], in_=seed[:])
+        nc.vector.tensor_tensor(out=slope[:], in0=seed[:], in1=seed[:], op=ALU.mult)
+        nc.vector.tensor_scalar(out=slope[:], in0=slope[:], scalar1=-EPS, scalar2=None, op0=ALU.mult)
+        nc.vector.tensor_scalar(out=neg_dt[:], in0=columns("dt", B_TILES), scalar1=-1.0, scalar2=None, op0=ALU.mult)
+        b_mod_cols = columns("b_mod", n_tiles)
+        b_tgt_cols = columns("b_tgt", n_tiles)
+        bias_cols = columns("bias", n_tiles)
+
+        ct_codes = keep.tile([P, PASSES, BATCH], U32, align_bytes=64)
+        ct_scales = keep.tile([P, PASSES, BATCH], U8, align_bytes=64)
+
+        def transpose_pass(g):
+            grouped = stage.tile([P, BATCH * PACK], BF16, align_bytes=64)
+            grouped_words = grouped[:].bitcast(F32).rearrange("p (b u) -> p b u", u=2)
+            for half in range(2):
+                flipped = flip_psum.tile([P, 2, 2 * P], F32, tag="flip")
+                for jj in range(2):
+                    words = c_sb[:, 2 * half + jj, :].bitcast(F32)
+                    for u in range(2):
+                        nc.tensor.transpose(
+                            flipped[:, u, P * jj : P * (jj + 1)],
+                            words[:, 2 * P * g + u : 2 * P * (g + 1) : 2],
+                            ident_f32[:],
+                        )
+                source = flipped[:].rearrange("p u b -> p b u")
+                target = grouped_words[:, 2 * P * half : 2 * P * (half + 1), :]
+                if half == 0:
+                    nc.vector.tensor_copy(out=target, in_=source)
+                else:
+                    nc.scalar.copy(out=target, in_=source)
+            return grouped
+
+        def quantise_pass(g, grouped):
+            nc.vector.quantize_mx(
+                out=ct_codes[:, g, :].bitcast(FP8X4), scales=ct_scales[:, g, :], in_=grouped[:]
+            )
+
+        waiting = None
+        for g in range(PASSES):
+            grouped = transpose_pass(g)
+            if waiting is not None:
+                quantise_pass(g - 1, waiting)
+            waiting = grouped
+        quantise_pass(PASSES - 1, waiting)
+
+        def weight_scale(w, g, cols):
+            if g < PLANES_PER_TILE:
+                return (planes_mod, planes_tgt)[w][4 * g : P, cols]
+            return planes_last[4 * w : P, cols]
+
+        def mx_group(w, i):
+            w_sb = (w_mod_sb, w_tgt_sb)[w]
+            cols = slice(P * i, P * (i + 1))
+            acc = mx_psum.tile([P, BATCH], F32, tag="acc")
+            for g in range(PASSES):
+                nc.tensor.matmul_mx(
+                    out=acc[:],
+                    lhsT=w_sb[:, g, cols].bitcast(FP8X4),
+                    lhsT_scale=weight_scale(w, g, cols),
+                    rhs=ct_codes[:, g, :].bitcast(FP8X4),
+                    rhs_scale=ct_scales[:, g, :],
+                    start=(g == 0),
+                    stop=(g == PASSES - 1),
+                )
+            return acc
+
+        def rate_of_round(r):
+            abs_f = work.tile([P, ROUND_TILES, BATCH], F32, tag="abs_f")
+            newton = work.tile([P, ROUND_TILES, BATCH], F32, tag="newton")
+            rate = work.tile([P, ROUND_TILES, BATCH], F32, tag="rate")
+            for ii in range(ROUND_TILES):
+                i = ROUND_TILES * r + ii
+                col = slice(i, i + 1)
+                acc = mx_group(0, i)
+                nc.scalar.activation(out=abs_f[:, ii, :], in_=acc[:], func=ACT.Tanh, bias=b_mod_cols[:, col])
+                nc.scalar.activation(out=abs_f[:, ii, :], in_=abs_f[:, ii, :], func=ACT.Abs)
+                nc.vector.tensor_scalar(
+                    out=newton[:, ii, :], in0=abs_f[:, ii, :], scalar1=slope[:, col], scalar2=seed[:, col],
+                    op0=ALU.mult, op1=ALU.add,
+                )
+                nc.vector.scalar_tensor_tensor(
+                    out=rate[:, ii, :], in0=abs_f[:, ii, :], scalar=inv_tau[:, col], in1=newton[:, ii, :],
+                    op0=ALU.add, op1=ALU.mult,
+                )
+            return rate
+
+        def goal_of_round(r):
+            goal = work.tile([P, ROUND_TILES, BATCH], F32, tag="goal")
+            for ii in range(ROUND_TILES):
+                i = ROUND_TILES * r + ii
+                col = slice(i, i + 1)
+                acc = mx_group(1, i)
+                nc.scalar.activation(out=goal[:, ii, :], in_=acc[:], func=ACT.Tanh, bias=b_tgt_cols[:, col])
+                nc.scalar.activation(out=goal[:, ii, :], in_=goal[:, ii, :], func=ACT.Identity, bias=bias_cols[:, col])
+            return goal
+
+        out_view = out.rearrange("(j p) n -> p j n", p=P)
+
+        def blend_round(r, rate, goal):
+            decay = work.tile([P, B_TILES, ROUND_COLS], F32, tag="decay")
+            pull = work.tile([P, B_TILES, ROUND_COLS], F32, tag="pull")
+            new_h = work.tile([P, B_TILES, ROUND_COLS], F32, tag="new_h", bufs=3)
+            flipped = []
+            for source in (rate, goal):
+                banks = []
+                for half in range(2):
+                    bank = flip_psum.tile([P, 2, ROUND_COLS], F32, tag="flip")
+                    banks.append(bank)
+                for ii in range(ROUND_TILES):
+                    for j in range(B_TILES):
+                        nc.tensor.transpose(
+                            banks[j // 2][:, j % 2, P * ii : P * (ii + 1)], source[:, ii, P * j : P * (j + 1)], ident_f32[:]
+                        )
+                flipped.append(banks)
+            rate_t, goal_t = flipped
+            h_cols = slice(IN + ROUND_COLS * r, IN + ROUND_COLS * (r + 1))
+            for j in range(B_TILES):
+                nc.scalar.activation(
+                    out=decay[:, j, :], in_=rate_t[j // 2][:, j % 2, :], func=ACT.Exp, scale=neg_dt[:, j : j + 1]
+                )
+            for half in range(2):
+                rows = slice(2 * half, 2 * half + 2)
+                nc.vector.tensor_tensor(
+                    out=pull[:, rows, :], in0=c_sb[:, rows, h_cols], in1=goal_t[half][:], op=ALU.subtract
+                )
+            for half in range(2):
+                rows = slice(2 * half, 2 * half + 2)
+                nc.vector.scalar_tensor_tensor(
+                    out=pull[:, rows, :], in0=decay[:, rows, :], scalar=-1.0, in1=pull[:, rows, :],
+                    op0=ALU.add, op1=ALU.mult,
+                )
+                nc.vector.tensor_tensor(out=new_h[:, rows, :], in0=c_sb[:, rows, h_cols], in1=pull[:, rows, :], op=ALU.add)
+                nc.sync.dma_start(
+                    out=out_view[:, rows, ROUND_COLS * r : ROUND_COLS * (r + 1)], in_=new_h[:, rows, :]
+                )
+
+        previous = None
+        for r in range(ROUNDS):
+            rate = rate_of_round(r)
+            if previous is not None:
+                blend_round(r - 1, previous[0], previous[1])
+            previous = (rate, goal_of_round(r))
+        blend_round(ROUNDS - 1, previous[0], previous[1])

@@ -46,40 +46,44 @@ def tile_ltccell_kernel(
         planes_mod = keep.tile([P, HID], U8, align_bytes=64)
         planes_tgt = keep.tile([P, HID], U8, align_bytes=64)
         planes_last = keep.tile([P, HID], U8, align_bytes=64)
-        for plane in (planes_mod, planes_tgt, planes_last):
+        vec_rows = keep.tile([P, P], BF16)
+        for plane in (planes_mod, planes_last, planes_tgt):
             nc.vector.memset(plane[:].bitcast(I32), 0)
+        nc.vector.memset(vec_rows[:], 0.0)
+
+        c_sb = keep.tile([P, B_TILES, K], BF16)
+        x_view = x.rearrange("(j p) k -> p j k", p=P)
+        h_view = h.rearrange("(j p) k -> p j k", p=P)
+        nc.scalar.dma_start(out=c_sb[:, :, 0:IN], in_=x_view)
+        for g in range(1, PASSES):
+            nc.scalar.dma_start(
+                out=c_sb[:, :, K_PASS * g : K_PASS * (g + 1)], in_=h_view[:, :, K_PASS * (g - 1) : K_PASS * g]
+            )
+
+        ident_f32 = keep.tile([P, P], F32)
+        make_identity(nc, ident_f32[:])
+        ident_bf16 = keep.tile([P, P], BF16)
+        nc.vector.tensor_copy(out=ident_bf16[:], in_=ident_f32[:])
 
         n_tiles = HID // P
-        vec_rows = keep.tile([P, P], BF16)
-        nc.vector.memset(vec_rows[:], 0.0)
         first_row = {}
         for position, (name, vec) in enumerate(
             (("b_mod", b_mod), ("b_tgt", b_tgt), ("log_tau", log_tau), ("bias", bias))
         ):
             first_row[name] = n_tiles * position
-            nc.scalar.dma_start(
+            nc.gpsimd.dma_start(
                 out=vec_rows[n_tiles * position : n_tiles * (position + 1), :],
                 in_=vec.rearrange("(r c) -> r c", c=P),
             )
         first_row["dt"] = 4 * n_tiles
-        nc.scalar.dma_start(
+        nc.gpsimd.dma_start(
             out=vec_rows[4 * n_tiles : 4 * n_tiles + B_TILES, :], in_=time_delta.rearrange("(r c) o -> r (c o)", c=P)
         )
 
-        c_sb = keep.tile([P, B_TILES, K], BF16)
-        x_view = x.rearrange("(j p) k -> p j k", p=P)
-        h_view = h.rearrange("(j p) k -> p j k", p=P)
-        nc.gpsimd.dma_start(out=c_sb[:, :, 0:IN], in_=x_view)
-        ident_f32 = keep.tile([P, P], F32)
-        make_identity(nc, ident_f32[:])
-        ident_bf16 = keep.tile([P, P], BF16)
-        nc.vector.tensor_copy(out=ident_bf16[:], in_=ident_f32[:])
-        for g in range(1, PASSES):
-            nc.gpsimd.dma_start(
-                out=c_sb[:, :, K_PASS * g : K_PASS * (g + 1)], in_=h_view[:, :, K_PASS * (g - 1) : K_PASS * g]
-            )
+        w_mod_sb = keep.tile([P, PASSES, HID], U32, align_bytes=64)
+        w_tgt_sb = keep.tile([P, PASSES, HID], U32, align_bytes=64)
 
-        for w, (scales, plane) in enumerate(((W_mod_scales, planes_mod), (W_tgt_scales, planes_tgt))):
+        def load_scales(w, scales, plane):
             for quad in range(4):
                 rows = slice(4 * quad, 4 * quad + 4)
                 nc.sync.dma_start(
@@ -91,16 +95,21 @@ def tile_ltccell_kernel(
                     in_=scales[PLANES_PER_TILE, rows, :].bitcast(I32),
                 )
 
-        w_mod_sb = keep.tile([P, PASSES, HID], U32, align_bytes=64)
-        w_tgt_sb = keep.tile([P, PASSES, HID], U32, align_bytes=64)
-        for r in range(ROUNDS):
-            for words, w_sb in ((W_mod_words, w_mod_sb), (W_tgt_words, w_tgt_sb)):
-                nc.sync.dma_start(
-                    out=w_sb[:, :, ROUND_COLS * r : ROUND_COLS * (r + 1)].bitcast(I32),
-                    in_=words.rearrange("g p n t -> p g (n t)")[
-                        :, :, PACK * ROUND_COLS * r : PACK * ROUND_COLS * (r + 1)
-                    ].bitcast(I32),
-                )
+        def load_words(r, words, w_sb):
+            nc.sync.dma_start(
+                out=w_sb[:, :, ROUND_COLS * r : ROUND_COLS * (r + 1)].bitcast(I32),
+                in_=words.rearrange("g p n t -> p g (n t)")[
+                    :, :, PACK * ROUND_COLS * r : PACK * ROUND_COLS * (r + 1)
+                ].bitcast(I32),
+            )
+
+        load_scales(0, W_mod_scales, planes_mod)
+        load_words(0, W_mod_words, w_mod_sb)
+        load_scales(1, W_tgt_scales, planes_tgt)
+        load_words(0, W_tgt_words, w_tgt_sb)
+        for r in range(1, ROUNDS):
+            load_words(r, W_mod_words, w_mod_sb)
+            load_words(r, W_tgt_words, w_tgt_sb)
 
         vec_ps = flip_psum.tile([P, P], BF16, tag="flip")
         nc.tensor.transpose(vec_ps[:], vec_rows[:], ident_bf16[:])

@@ -111,28 +111,6 @@ def tile_ltccell_kernel(
             load_words(r, W_mod_words, w_mod_sb)
             load_words(r, W_tgt_words, w_tgt_sb)
 
-        vec_ps = flip_psum.tile([P, P], BF16, tag="flip")
-        nc.tensor.transpose(vec_ps[:], vec_rows[:], ident_bf16[:])
-        vec_cols = keep.tile([P, P], F32)
-        nc.vector.tensor_copy(out=vec_cols[:], in_=vec_ps[:])
-
-        def columns(name, count):
-            return vec_cols[:, first_row[name] : first_row[name] + count]
-
-        inv_tau = keep.tile([P, n_tiles], F32)
-        seed = keep.tile([P, n_tiles], F32)
-        slope = keep.tile([P, n_tiles], F32)
-        neg_dt = keep.tile([P, B_TILES], F32)
-        nc.scalar.activation(out=inv_tau[:], in_=columns("log_tau", n_tiles), func=ACT.Exp, scale=-1.0)
-        nc.vector.tensor_scalar(out=seed[:], in0=inv_tau[:], scalar1=EPS, scalar2=1.0, op0=ALU.mult, op1=ALU.add)
-        nc.vector.reciprocal(out=seed[:], in_=seed[:])
-        nc.vector.tensor_tensor(out=slope[:], in0=seed[:], in1=seed[:], op=ALU.mult)
-        nc.vector.tensor_scalar(out=slope[:], in0=slope[:], scalar1=-EPS, scalar2=None, op0=ALU.mult)
-        nc.vector.tensor_scalar(out=neg_dt[:], in0=columns("dt", B_TILES), scalar1=-1.0, scalar2=None, op0=ALU.mult)
-        b_mod_cols = columns("b_mod", n_tiles)
-        b_tgt_cols = columns("b_tgt", n_tiles)
-        bias_cols = columns("bias", n_tiles)
-
         ct_codes = keep.tile([P, PASSES, BATCH], U32, align_bytes=64)
         ct_scales = keep.tile([P, PASSES, BATCH], U8, align_bytes=64)
 
@@ -169,6 +147,28 @@ def tile_ltccell_kernel(
                 quantise_pass(g - 1, waiting)
             waiting = grouped
         quantise_pass(PASSES - 1, waiting)
+
+        vec_ps = flip_psum.tile([P, P], BF16, tag="flip")
+        nc.tensor.transpose(vec_ps[:], vec_rows[:], ident_bf16[:])
+        vec_cols = keep.tile([P, P], F32)
+        nc.vector.tensor_copy(out=vec_cols[:], in_=vec_ps[:])
+
+        def columns(name, count):
+            return vec_cols[:, first_row[name] : first_row[name] + count]
+
+        inv_tau = keep.tile([P, n_tiles], F32)
+        seed = keep.tile([P, n_tiles], F32)
+        slope = keep.tile([P, n_tiles], F32)
+        neg_dt = keep.tile([P, B_TILES], F32)
+        nc.scalar.activation(out=inv_tau[:], in_=columns("log_tau", n_tiles), func=ACT.Exp, scale=-1.0)
+        nc.vector.tensor_scalar(out=seed[:], in0=inv_tau[:], scalar1=EPS, scalar2=1.0, op0=ALU.mult, op1=ALU.add)
+        nc.vector.reciprocal(out=seed[:], in_=seed[:])
+        nc.vector.tensor_tensor(out=slope[:], in0=seed[:], in1=seed[:], op=ALU.mult)
+        nc.vector.tensor_scalar(out=slope[:], in0=slope[:], scalar1=-EPS, scalar2=None, op0=ALU.mult)
+        nc.vector.tensor_scalar(out=neg_dt[:], in0=columns("dt", B_TILES), scalar1=-1.0, scalar2=None, op0=ALU.mult)
+        b_mod_cols = columns("b_mod", n_tiles)
+        b_tgt_cols = columns("b_tgt", n_tiles)
+        bias_cols = columns("bias", n_tiles)
 
         def weight_scale(w, g, cols):
             if g < PLANES_PER_TILE:

@@ -24,6 +24,7 @@ B_TILES = BATCH // P
 ROUND_TILES = 2
 ROUND_COLS = ROUND_TILES * P
 ROUNDS = HID // ROUND_COLS
+H_LOADS = 2
 PLANES_PER_TILE = 4
 EPS = 1e-6
 
@@ -55,10 +56,9 @@ def tile_ltccell_kernel(
         x_view = x.rearrange("(j p) k -> p j k", p=P)
         h_view = h.rearrange("(j p) k -> p j k", p=P)
         nc.scalar.dma_start(out=c_sb[:, :, 0:IN], in_=x_view)
-        for g in range(1, PASSES):
-            nc.scalar.dma_start(
-                out=c_sb[:, :, K_PASS * g : K_PASS * (g + 1)], in_=h_view[:, :, K_PASS * (g - 1) : K_PASS * g]
-            )
+        for part in range(H_LOADS):
+            cols = slice(HID // H_LOADS * part, HID // H_LOADS * (part + 1))
+            nc.scalar.dma_start(out=c_sb[:, :, IN:K][:, :, cols], in_=h_view[:, :, cols])
 
         ident_f32 = keep.tile([P, P], F32)
         make_identity(nc, ident_f32[:])

@@ -20,12 +20,14 @@ IN = 512
 HID = 2048
 K = IN + HID
 PASSES = K // K_PASS
-B_TILES = BATCH // P
-ROUND_TILES = 2
-ROUND_COLS = ROUND_TILES * P
-ROUNDS = HID // ROUND_COLS
-H_LOADS = 2
+TILES = BATCH // P
+COLS = 512
+BLOCKS = HID // COLS
+ROUNDS = ((0, 512), (512, 512), (1024, 512), (1536, 256), (1792, 256))
+U_TILES = HID // P
+HEAD_TILES = 4
 PLANES_PER_TILE = 4
+WARM_UP = 5
 EPS = 1e-6
 
 FLOPS = 2 * 2 * BATCH * K * HID
@@ -38,81 +40,114 @@ def tile_ltccell_kernel(
     with ExitStack() as ctx:
         keep = ctx.enter_context(tc.tile_pool(name="keep", bufs=1))
         stage = ctx.enter_context(tc.tile_pool(name="stage", bufs=2))
-        work = ctx.enter_context(tc.tile_pool(name="work", bufs=2))
-        mx_psum = ctx.enter_context(tc.psum_pool(name="mx_psum", bufs=4))
+        work = ctx.enter_context(tc.tile_pool(name="work", bufs=4))
+        acc_psum = ctx.enter_context(tc.psum_pool(name="acc_psum", bufs=4))
         flip_psum = ctx.enter_context(tc.psum_pool(name="flip_psum", bufs=4))
         ctx.enter_context(tc.manual_schedule())
 
+        planes_mod = keep.tile([P, HID], U8, align_bytes=256)
+        planes_tgt = keep.tile([P, HID], U8, align_bytes=256)
+        last_mod = keep.tile([P, HID], U8, align_bytes=256)
+        last_tgt = keep.tile([P, HID], U8, align_bytes=256)
+        row_vecs = keep.tile([P, COLS], BF16)
+        unit_rows = keep.tile([P, P], BF16)
+        dt_sb = keep.tile([P, TILES], BF16)
+        warm = keep.tile([P, 1], F32)
+        zeros = keep.tile([P, COLS], BF16)
+        nc.vector.memset(zeros[:], 0.0)
+        nc.vector.memset(row_vecs[:], 0.0)
+        nc.vector.memset(warm[:], 0.0)
+        nc.vector.memset(planes_mod[:].bitcast(I32), 0)
+        nc.vector.memset(unit_rows[:], 0.0)
+        nc.vector.memset(last_mod[:].bitcast(I32), 0)
+        nc.vector.memset(planes_tgt[:].bitcast(I32), 0)
+        nc.vector.memset(last_tgt[:].bitcast(I32), 0)
 
-        planes_mod = keep.tile([P, HID], U8, align_bytes=64)
-        planes_tgt = keep.tile([P, HID], U8, align_bytes=64)
-        planes_last = keep.tile([P, HID], U8, align_bytes=64)
-        vec_rows = keep.tile([P, P], BF16)
-        for plane in (planes_mod, planes_last, planes_tgt):
-            nc.vector.memset(plane[:].bitcast(I32), 0)
-        nc.vector.memset(vec_rows[:], 0.0)
+        x_sb = keep.tile([P, TILES, IN], BF16)
+        h_sb = keep.tile([P, TILES, HID], BF16)
+        x_view = x.rearrange("(p j) k -> p j k", j=TILES)
+        h_view = h.rearrange("(p j) k -> p j k", j=TILES)
+        out_view = out.rearrange("(p j) n -> p j n", j=TILES)
 
-        c_sb = keep.tile([P, B_TILES, K], BF16)
-        x_view = x.rearrange("(j p) k -> p j k", p=P)
-        h_view = h.rearrange("(j p) k -> p j k", p=P)
-        nc.scalar.dma_start(out=c_sb[:, :, 0:IN], in_=x_view)
-        for part in range(H_LOADS):
-            cols = slice(HID // H_LOADS * part, HID // H_LOADS * (part + 1))
-            nc.scalar.dma_start(out=c_sb[:, :, IN:K][:, :, cols], in_=h_view[:, :, cols])
+        w_mod_sb = keep.tile([P, PASSES, HID], U32, align_bytes=256)
+        w_tgt_sb = keep.tile([P, PASSES, HID], U32, align_bytes=256)
+
+        def load_h(first, last):
+            nc.sync.dma_start(out=h_sb[:, :, first:last], in_=h_view[:, :, first:last])
+
+        def load_scales(scales, planes):
+            for quad in range(4):
+                nc.sync.dma_start(
+                    out=planes[32 * quad : 32 * quad + 16, :].bitcast(I32),
+                    in_=scales[0:PLANES_PER_TILE, 4 * quad : 4 * quad + 4, :].bitcast(I32),
+                )
+
+        def load_last_scales(scales, plane):
+            for quad in range(4):
+                nc.sync.dma_start(
+                    out=plane[32 * quad : 32 * quad + 4, :].bitcast(I32),
+                    in_=scales[PLANES_PER_TILE, 4 * quad : 4 * quad + 4, :].bitcast(I32),
+                )
+
+        def load_words(words, w_sb, first, width, passes):
+            last = first + width
+            nc.sync.dma_start(
+                out=w_sb[:, passes, first:last].bitcast(I32),
+                in_=words.rearrange("g p n t -> p g (n t)")[:, passes, PACK * first : PACK * last].bitcast(I32),
+            )
+
+        nc.scalar.dma_start(out=row_vecs[0:BLOCKS, :], in_=bias.rearrange("(r c) -> r c", c=COLS))
+        nc.scalar.activation(out=warm[:], in_=warm[:], func=ACT.Exp)
+        nc.sync.dma_start(out=x_sb[:], in_=x_view)
+        load_scales(W_mod_scales, planes_mod)
+        load_h(0, K_PASS)
+        load_words(W_mod_words, w_mod_sb, 0, COLS, slice(0, 1))
+        load_h(K_PASS, 2 * K_PASS)
+        load_words(W_mod_words, w_mod_sb, 0, COLS, slice(1, 2))
+        load_last_scales(W_mod_scales, last_mod)
+        load_h(2 * K_PASS, 3 * K_PASS)
+        load_words(W_mod_words, w_mod_sb, 0, COLS, slice(2, 3))
+        load_h(3 * K_PASS, 4 * K_PASS)
+        load_words(W_mod_words, w_mod_sb, 0, COLS, slice(3, 5))
+        load_scales(W_tgt_scales, planes_tgt)
+        load_words(W_tgt_words, w_tgt_sb, 0, COLS, slice(0, 5))
+        for half in range(2):
+            load_words(W_mod_words, w_mod_sb, COLS + COLS // 2 * half, COLS // 2, slice(0, 5))
+        load_last_scales(W_tgt_scales, last_tgt)
+        load_words(W_tgt_words, w_tgt_sb, COLS, COLS, slice(0, 5))
+        for block in range(2, BLOCKS):
+            load_words(W_mod_words, w_mod_sb, COLS * block, COLS, slice(0, 5))
+            load_words(W_tgt_words, w_tgt_sb, COLS * block, COLS, slice(0, 5))
 
         ident_f32 = keep.tile([P, P], F32)
         make_identity(nc, ident_f32[:])
         ident_bf16 = keep.tile([P, P], BF16)
         nc.vector.tensor_copy(out=ident_bf16[:], in_=ident_f32[:])
-
         n_tiles = HID // P
-        first_row = {}
-        for position, (name, vec) in enumerate(
-            (("b_mod", b_mod), ("b_tgt", b_tgt), ("log_tau", log_tau), ("bias", bias))
-        ):
-            first_row[name] = n_tiles * position
-            nc.gpsimd.dma_start(
-                out=vec_rows[n_tiles * position : n_tiles * (position + 1), :],
-                in_=vec.rearrange("(r c) -> r c", c=P),
-            )
-        first_row["dt"] = 4 * n_tiles
-        nc.gpsimd.dma_start(
-            out=vec_rows[4 * n_tiles : 4 * n_tiles + B_TILES, :], in_=time_delta.rearrange("(r c) o -> r (c o)", c=P)
-        )
+        nc.gpsimd.dma_start(out=row_vecs[BLOCKS : 2 * BLOCKS, :], in_=b_tgt.rearrange("(r c) -> r c", c=COLS))
+        nc.gpsimd.dma_start(out=unit_rows[0:n_tiles, :], in_=b_mod.rearrange("(r c) -> r c", c=P))
+        nc.gpsimd.dma_start(out=unit_rows[n_tiles : 2 * n_tiles, :], in_=log_tau.rearrange("(r c) -> r c", c=P))
+        nc.gpsimd.dma_start(out=dt_sb[:], in_=time_delta.rearrange("(p j) o -> p (j o)", j=TILES))
 
-        w_mod_sb = keep.tile([P, PASSES, HID], U32, align_bytes=64)
-        w_tgt_sb = keep.tile([P, PASSES, HID], U32, align_bytes=64)
+        bias_all = keep.tile([P, HID], BF16)
+        b_tgt_all = keep.tile([P, HID], BF16)
 
-        def load_scales(w, scales, plane):
-            for quad in range(4):
-                rows = slice(4 * quad, 4 * quad + 4)
-                nc.sync.dma_start(
-                    out=plane[32 * quad : 32 * quad + 16, :].bitcast(I32),
-                    in_=scales[0:PLANES_PER_TILE, rows, :].bitcast(I32),
-                )
-                nc.sync.dma_start(
-                    out=planes_last[32 * quad + 4 * w : 32 * quad + 4 * w + 4, :].bitcast(I32),
-                    in_=scales[PLANES_PER_TILE, rows, :].bitcast(I32),
-                )
+        def spread(first_row, target):
+            for pair in range(BLOCKS // 2):
+                spread_ps = flip_psum.tile([P, 2 * COLS], BF16, tag="flip")
+                for part in range(2):
+                    row = first_row + 2 * pair + part
+                    nc.tensor.matmul(
+                        spread_ps[:, COLS * part : COLS * (part + 1)],
+                        lhsT=ident_bf16[:, row : row + 1].to_broadcast([P, P]),
+                        rhs=row_vecs[:],
+                        start=True,
+                        stop=True,
+                    )
+                nc.scalar.copy(out=target[:, 2 * COLS * pair : 2 * COLS * (pair + 1)], in_=spread_ps[:])
 
-        def load_words(r, words, w_sb):
-            nc.sync.dma_start(
-                out=w_sb[:, :, ROUND_COLS * r : ROUND_COLS * (r + 1)].bitcast(I32),
-                in_=words.rearrange("g p n t -> p g (n t)")[
-                    :, :, PACK * ROUND_COLS * r : PACK * ROUND_COLS * (r + 1)
-                ].bitcast(I32),
-            )
-
-        load_scales(0, W_mod_scales, planes_mod)
-        load_words(0, W_mod_words, w_mod_sb)
-        load_scales(1, W_tgt_scales, planes_tgt)
-        load_words(0, W_tgt_words, w_tgt_sb)
-        for r in range(1, ROUNDS):
-            load_words(r, W_mod_words, w_mod_sb)
-            load_words(r, W_tgt_words, w_tgt_sb)
-
-        ct_codes = keep.tile([P, PASSES, BATCH], U32, align_bytes=64)
-        ct_scales = keep.tile([P, PASSES, BATCH], U8, align_bytes=64)
+        ct_codes = keep.tile([P, PASSES, BATCH], U32, align_bytes=256)
+        ct_scales = keep.tile([P, PASSES, BATCH], U8, align_bytes=256)
 
         def transpose_pass(g):
             grouped = stage.tile([P, BATCH * PACK], BF16, align_bytes=64)
@@ -120,151 +155,222 @@ def tile_ltccell_kernel(
             for half in range(2):
                 flipped = flip_psum.tile([P, 2, 2 * P], F32, tag="flip")
                 for jj in range(2):
-                    words = c_sb[:, 2 * half + jj, :].bitcast(F32)
+                    j = 2 * half + jj
+                    if g == 0:
+                        words = x_sb[:, j, :].bitcast(F32)
+                    else:
+                        words = h_sb[:, j, K_PASS * (g - 1) : K_PASS * g].bitcast(F32)
                     for u in range(2):
-                        nc.tensor.transpose(
-                            flipped[:, u, P * jj : P * (jj + 1)],
-                            words[:, 2 * P * g + u : 2 * P * (g + 1) : 2],
-                            ident_f32[:],
-                        )
+                        nc.tensor.transpose(flipped[:, u, P * jj : P * (jj + 1)], words[:, u : 2 * P : 2], ident_f32[:])
                 source = flipped[:].rearrange("p u b -> p b u")
                 target = grouped_words[:, 2 * P * half : 2 * P * (half + 1), :]
-                if half == 0:
-                    nc.vector.tensor_copy(out=target, in_=source)
-                else:
-                    nc.scalar.copy(out=target, in_=source)
+                nc.scalar.copy(out=target, in_=source)
             return grouped
 
         def quantise_pass(g, grouped):
-            nc.vector.quantize_mx(
-                out=ct_codes[:, g, :].bitcast(FP8X4), scales=ct_scales[:, g, :], in_=grouped[:]
-            )
-
-        waiting = None
-        for g in range(PASSES):
-            grouped = transpose_pass(g)
-            if waiting is not None:
-                quantise_pass(g - 1, waiting)
-            waiting = grouped
-        quantise_pass(PASSES - 1, waiting)
-
-        vec_ps = flip_psum.tile([P, P], BF16, tag="flip")
-        nc.tensor.transpose(vec_ps[:], vec_rows[:], ident_bf16[:])
-        vec_cols = keep.tile([P, P], F32)
-        nc.vector.tensor_copy(out=vec_cols[:], in_=vec_ps[:])
-
-        def columns(name, count):
-            return vec_cols[:, first_row[name] : first_row[name] + count]
-
-        inv_tau = keep.tile([P, n_tiles], F32)
-        seed = keep.tile([P, n_tiles], F32)
-        slope = keep.tile([P, n_tiles], F32)
-        neg_dt = keep.tile([P, B_TILES], F32)
-        nc.scalar.activation(out=inv_tau[:], in_=columns("log_tau", n_tiles), func=ACT.Exp, scale=-1.0)
-        nc.vector.tensor_scalar(out=seed[:], in0=inv_tau[:], scalar1=EPS, scalar2=1.0, op0=ALU.mult, op1=ALU.add)
-        nc.vector.reciprocal(out=seed[:], in_=seed[:])
-        nc.vector.tensor_tensor(out=slope[:], in0=seed[:], in1=seed[:], op=ALU.mult)
-        nc.vector.tensor_scalar(out=slope[:], in0=slope[:], scalar1=-EPS, scalar2=None, op0=ALU.mult)
-        nc.vector.tensor_scalar(out=neg_dt[:], in0=columns("dt", B_TILES), scalar1=-1.0, scalar2=None, op0=ALU.mult)
-        b_mod_cols = columns("b_mod", n_tiles)
-        b_tgt_cols = columns("b_tgt", n_tiles)
-        bias_cols = columns("bias", n_tiles)
+            nc.vector.quantize_mx(out=ct_codes[:, g, :].bitcast(FP8X4), scales=ct_scales[:, g, :], in_=grouped[:])
 
         def weight_scale(w, g, cols):
             if g < PLANES_PER_TILE:
                 return (planes_mod, planes_tgt)[w][4 * g : P, cols]
-            return planes_last[4 * w : P, cols]
+            return (last_mod, last_tgt)[w][:, cols]
 
-        def mx_group(w, i):
-            w_sb = (w_mod_sb, w_tgt_sb)[w]
+        def f_pass(acc, i, g):
             cols = slice(P * i, P * (i + 1))
-            acc = mx_psum.tile([P, BATCH], F32, tag="acc")
+            nc.tensor.matmul_mx(
+                out=acc[:],
+                lhsT=w_mod_sb[:, g, cols].bitcast(FP8X4),
+                lhsT_scale=weight_scale(0, g, cols),
+                rhs=ct_codes[:, g, :].bitcast(FP8X4),
+                rhs_scale=ct_scales[:, g, :],
+                start=(g == 0),
+                stop=(g == PASSES - 1),
+            )
+
+        def a_pass(acc, cols, j, g):
+            rows = slice(P * j, P * (j + 1))
+            nc.tensor.matmul_mx(
+                out=acc,
+                lhsT=ct_codes[:, g, rows].bitcast(FP8X4),
+                lhsT_scale=ct_scales[:, g, rows],
+                rhs=w_tgt_sb[:, g, cols].bitcast(FP8X4),
+                rhs_scale=weight_scale(1, g, cols),
+                start=(g == 0),
+                stop=(g == PASSES - 1),
+            )
+
+        tiles = [(r, j) for r in range(len(ROUNDS)) for j in range(TILES)]
+        h_less_bias = keep.tile([P, TILES, HID], F32)
+        less_bias_left = [(block, j) for block in range(BLOCKS) for j in range(TILES)]
+        goal, decay, rates, abs_v, flips = {}, {}, {}, {}, {}
+
+        def units(r):
+            first, width = ROUNDS[r]
+            return slice(first, first + width)
+
+        def less_bias():
+            block, j = less_bias_left.pop(0)
+            cols = slice(COLS * block, COLS * (block + 1))
+            nc.vector.tensor_tensor(
+                out=h_less_bias[:, j, cols], in0=h_sb[:, j, cols], in1=bias_all[:, cols], op=ALU.subtract
+            )
+
+        def add_b_tgt(n, acc):
+            r, j = tiles[n]
+            goal[n] = work.tile([P, ROUNDS[r][1]], F32, tag="goal", bufs=7, name="goal")
+            nc.vector.tensor_tensor(out=goal[n][:], in0=acc, in1=b_tgt_all[:, units(r)], op=ALU.add)
+
+        def tanh_goal(n):
+            nc.scalar.activation(out=goal[n][:], in_=goal[n][:], func=ACT.Tanh)
+
+        def pull(n):
+            r, j = tiles[n]
+            nc.vector.tensor_tensor(
+                out=goal[n][:], in0=goal[n][:], in1=h_less_bias[:, j, units(r)], op=ALU.subtract
+            )
+
+        def decay_of(n):
+            r, j = tiles[n]
+            decay[n] = work.tile([P, ROUNDS[r][1]], F32, tag="decay", bufs=6, name="decay")
+            nc.scalar.activation(out=decay[n][:], in_=flips[n][:], func=ACT.Exp, scale=neg_dt[:, j : j + 1])
+
+        def shrink(n):
+            nc.vector.scalar_tensor_tensor(
+                out=goal[n][:], in0=decay[n][:], scalar=-1.0, in1=goal[n][:], op0=ALU.add, op1=ALU.mult
+            )
+
+        def finish(n):
+            r, j = tiles[n]
+            new_h = work.tile([P, ROUNDS[r][1]], F32, tag="new_h", bufs=4, name="new_h")
+            nc.vector.tensor_tensor(out=new_h[:], in0=h_sb[:, j, units(r)], in1=goal[n][:], op=ALU.subtract)
+            nc.sync.dma_start(out=out_view[:, j, units(r)], in_=new_h[:])
+
+        def abs_of(i, acc):
+            abs_v[i] = work.tile([P, BATCH], F32, tag="abs_v", bufs=5, name="abs_v")
+            nc.scalar.activation(out=abs_v[i][:], in_=acc[:], func=ACT.Abs, bias=b_mod_cols[:, i : i + 1])
+
+        def tanh_f(i):
+            nc.scalar.activation(out=abs_v[i][:], in_=abs_v[i][:], func=ACT.Tanh, bias=EPS)
+
+        def rate_of(i):
+            rates[i] = work.tile([P, BATCH], F32, tag="rate", bufs=6, name="rate")
+            nc.vector.tensor_scalar(
+                out=rates[i][:], in0=abs_v[i][:], scalar1=slope[:, i : i + 1], scalar2=base[:, i : i + 1],
+                op0=ALU.mult, op1=ALU.add,
+            )
+
+        def flip_rates(r):
+            first, width = ROUNDS[r]
+            for j in range(TILES):
+                flip = flip_psum.tile([P, width], F32, tag="flip", name="flip")
+                for ii in range(width // P):
+                    nc.tensor.transpose(
+                        flip[:, P * ii : P * (ii + 1)], rates[first // P + ii][:, P * j : P * (j + 1)], ident_f32[:]
+                    )
+                flips[TILES * r + j] = flip
+
+        accs = [acc_psum.tile([P, BATCH], F32, tag="acc", name="acc") for i in range(HEAD_TILES)]
+
+        def head_pass(g):
+            for i in range(HEAD_TILES):
+                f_pass(accs[i], i, g)
+
+        idle_ps = flip_psum.tile([P, COLS], F32, tag="flip")
+        for n in range(WARM_UP):
+            nc.tensor.matmul(idle_ps[:], lhsT=zeros[:, 0:P], rhs=zeros[:], start=True, stop=True)
+        grouped = transpose_pass(0)
+        spread(0, bias_all)
+        for g in range(1, PASSES):
+            quantise_pass(g - 1, grouped)
+            grouped = transpose_pass(g)
+            for n in range(3):
+                less_bias()
+            if g == PASSES - 1:
+                spread(BLOCKS, b_tgt_all)
+            head_pass(g - 1)
+        quantise_pass(PASSES - 1, grouped)
+
+        unit_ps = flip_psum.tile([P, P], BF16, tag="flip")
+        nc.tensor.transpose(unit_ps[:], unit_rows[:], ident_bf16[:])
+        unit_cols = keep.tile([P, 2 * n_tiles], F32)
+        nc.vector.tensor_copy(out=unit_cols[:], in_=unit_ps[:, 0 : 2 * n_tiles])
+        b_mod_cols = unit_cols[:, 0:n_tiles]
+
+        inv_tau = keep.tile([P, n_tiles], F32)
+        seed = keep.tile([P, n_tiles], F32)
+        slope = keep.tile([P, n_tiles], F32)
+        base = keep.tile([P, n_tiles], F32)
+        neg_dt = keep.tile([P, TILES], F32)
+        nc.scalar.activation(out=inv_tau[:], in_=unit_cols[:, n_tiles : 2 * n_tiles], func=ACT.Exp, scale=-1.0)
+        nc.vector.tensor_scalar(out=neg_dt[:], in0=dt_sb[:], scalar1=-1.0, scalar2=None, op0=ALU.mult)
+        nc.vector.tensor_scalar(out=seed[:], in0=inv_tau[:], scalar1=EPS, scalar2=1.0, op0=ALU.mult, op1=ALU.add)
+        nc.vector.reciprocal(out=seed[:], in_=seed[:])
+        nc.vector.tensor_tensor(out=slope[:], in0=seed[:], in1=seed[:], op=ALU.mult)
+        nc.vector.tensor_tensor(out=base[:], in0=seed[:], in1=inv_tau[:], op=ALU.mult)
+        nc.vector.scalar_tensor_tensor(
+            out=base[:], in0=slope[:], scalar=-EPS, in1=base[:], op0=ALU.mult, op1=ALU.add
+        )
+        head_pass(PASSES - 1)
+
+        for i in range(HEAD_TILES):
+            abs_of(i, accs[i])
+        while less_bias_left:
+            less_bias()
+
+        def f_group(i):
+            acc = acc_psum.tile([P, BATCH], F32, tag="acc", name="acc")
             for g in range(PASSES):
-                nc.tensor.matmul_mx(
-                    out=acc[:],
-                    lhsT=w_sb[:, g, cols].bitcast(FP8X4),
-                    lhsT_scale=weight_scale(w, g, cols),
-                    rhs=ct_codes[:, g, :].bitcast(FP8X4),
-                    rhs_scale=ct_scales[:, g, :],
-                    start=(g == 0),
-                    stop=(g == PASSES - 1),
-                )
+                f_pass(acc, i, g)
             return acc
 
-        def rate_of_round(r):
-            abs_f = work.tile([P, ROUND_TILES, BATCH], F32, tag="abs_f")
-            newton = work.tile([P, ROUND_TILES, BATCH], F32, tag="newton")
-            rate = work.tile([P, ROUND_TILES, BATCH], F32, tag="rate")
-            for ii in range(ROUND_TILES):
-                i = ROUND_TILES * r + ii
-                col = slice(i, i + 1)
-                acc = mx_group(0, i)
-                nc.scalar.activation(out=abs_f[:, ii, :], in_=acc[:], func=ACT.Tanh, bias=b_mod_cols[:, col])
-                nc.scalar.activation(out=abs_f[:, ii, :], in_=abs_f[:, ii, :], func=ACT.Abs)
-                nc.vector.tensor_scalar(
-                    out=newton[:, ii, :], in0=abs_f[:, ii, :], scalar1=slope[:, col], scalar2=seed[:, col],
-                    op0=ALU.mult, op1=ALU.add,
-                )
-                nc.vector.scalar_tensor_tensor(
-                    out=rate[:, ii, :], in0=abs_f[:, ii, :], scalar=inv_tau[:, col], in1=newton[:, ii, :],
-                    op0=ALU.add, op1=ALU.mult,
-                )
-            return rate
+        def a_group(n):
+            r, j = tiles[n]
+            acc = acc_psum.tile([P, COLS], F32, tag="acc", name="acc")
+            part = acc[:, 0 : ROUNDS[r][1]]
+            for g in range(PASSES):
+                a_pass(part, units(r), j, g)
+            return part
 
-        def goal_of_round(r):
-            goal = work.tile([P, ROUND_TILES, BATCH], F32, tag="goal")
-            for ii in range(ROUND_TILES):
-                i = ROUND_TILES * r + ii
-                col = slice(i, i + 1)
-                acc = mx_group(1, i)
-                nc.scalar.activation(out=goal[:, ii, :], in_=acc[:], func=ACT.Tanh, bias=b_tgt_cols[:, col])
-                nc.scalar.activation(out=goal[:, ii, :], in_=goal[:, ii, :], func=ACT.Identity, bias=bias_cols[:, col])
-            return goal
-
-        out_view = out.rearrange("(j p) n -> p j n", p=P)
-
-        def blend_round(r, rate, goal):
-            decay = work.tile([P, B_TILES, ROUND_COLS], F32, tag="decay")
-            pull = work.tile([P, B_TILES, ROUND_COLS], F32, tag="pull")
-            new_h = work.tile([P, B_TILES, ROUND_COLS], F32, tag="new_h", bufs=3)
-            flipped = []
-            for source in (rate, goal):
-                banks = []
-                for half in range(2):
-                    bank = flip_psum.tile([P, 2, ROUND_COLS], F32, tag="flip")
-                    banks.append(bank)
-                for ii in range(ROUND_TILES):
-                    for j in range(B_TILES):
-                        nc.tensor.transpose(
-                            banks[j // 2][:, j % 2, P * ii : P * (ii + 1)], source[:, ii, P * j : P * (j + 1)], ident_f32[:]
-                        )
-                flipped.append(banks)
-            rate_t, goal_t = flipped
-            h_cols = slice(IN + ROUND_COLS * r, IN + ROUND_COLS * (r + 1))
-            for j in range(B_TILES):
-                nc.scalar.activation(
-                    out=decay[:, j, :], in_=rate_t[j // 2][:, j % 2, :], func=ACT.Exp, scale=neg_dt[:, j : j + 1]
-                )
-            for half in range(2):
-                rows = slice(2 * half, 2 * half + 2)
-                nc.vector.tensor_tensor(
-                    out=pull[:, rows, :], in0=c_sb[:, rows, h_cols], in1=goal_t[half][:], op=ALU.subtract
-                )
-            for half in range(2):
-                rows = slice(2 * half, 2 * half + 2)
-                nc.vector.scalar_tensor_tensor(
-                    out=pull[:, rows, :], in0=decay[:, rows, :], scalar=-1.0, in1=pull[:, rows, :],
-                    op0=ALU.add, op1=ALU.mult,
-                )
-                nc.vector.tensor_tensor(out=new_h[:, rows, :], in0=c_sb[:, rows, h_cols], in1=pull[:, rows, :], op=ALU.add)
-                nc.sync.dma_start(
-                    out=out_view[:, rows, ROUND_COLS * r : ROUND_COLS * (r + 1)], in_=new_h[:, rows, :]
-                )
-
-        previous = None
-        for r in range(ROUNDS):
-            rate = rate_of_round(r)
-            if previous is not None:
-                blend_round(r - 1, previous[0], previous[1])
-            previous = (rate, goal_of_round(r))
-        blend_round(ROUNDS - 1, previous[0], previous[1])
+        f_after = {n: n + HEAD_TILES for n in range(10)}
+        f_after[11] = 14
+        f_after[13] = 15
+        flip_after = {1: 0, 5: 1, 9: 2, 13: 3, 17: 4}
+        f_waiting = list(range(HEAD_TILES))
+        to_decay, decayed = [], []
+        for n in range(len(tiles)):
+            acc = a_group(n)
+            for m in to_decay[0:2]:
+                decay_of(m)
+            decayed += to_decay[0:2]
+            to_decay = to_decay[2:]
+            for i in f_waiting:
+                tanh_f(i)
+            add_b_tgt(n, acc)
+            tanh_goal(n)
+            count = 2 if n > 13 else 1
+            blends = [m for m in decayed[0:count] if m < n - 1]
+            decayed = decayed[len(blends) :]
+            for m in blends:
+                shrink(m)
+            if n > 0:
+                pull(n - 1)
+            for i in f_waiting:
+                rate_of(i)
+            for m in blends:
+                finish(m)
+            f_waiting = []
+            if n in f_after:
+                i = f_after[n]
+                abs_of(i, f_group(i))
+                f_waiting = [i]
+            if n in flip_after:
+                r = flip_after[n]
+                flip_rates(r)
+                to_decay = to_decay + list(range(TILES * r, TILES * (r + 1)))
+        pull(len(tiles) - 1)
+        for m in to_decay:
+            decay_of(m)
+        for m in decayed + to_decay:
+            shrink(m)
+        for m in decayed + to_decay:
+            finish(m)

@@ -20,14 +20,13 @@ IN = 512
 HID = 2048
 K = IN + HID
 PASSES = K // K_PASS
-TILES = BATCH // P
-COLS = 512
-BLOCKS = HID // COLS
-ROUNDS = ((0, 512), (512, 512), (1024, 512), (1536, 256), (1792, 256))
+B_TILES = BATCH // P
 U_TILES = HID // P
+BANK = 512
+ROUNDS = ((0, 512), (512, 512), (1024, 512), (1536, 256), (1792, 256))
 HEAD_TILES = 4
 PLANES_PER_TILE = 4
-WARM_UP = 5
+VECTOR_RATES = 10
 EPS = 1e-6
 
 FLOPS = 2 * 2 * BATCH * K * HID
@@ -39,8 +38,6 @@ def tile_ltccell_kernel(
     nc = tc.nc
     with ExitStack() as ctx:
         keep = ctx.enter_context(tc.tile_pool(name="keep", bufs=1))
-        stage = ctx.enter_context(tc.tile_pool(name="stage", bufs=2))
-        work = ctx.enter_context(tc.tile_pool(name="work", bufs=4))
         acc_psum = ctx.enter_context(tc.psum_pool(name="acc_psum", bufs=4))
         flip_psum = ctx.enter_context(tc.psum_pool(name="flip_psum", bufs=4))
         ctx.enter_context(tc.manual_schedule())
@@ -49,31 +46,28 @@ def tile_ltccell_kernel(
         planes_tgt = keep.tile([P, HID], U8, align_bytes=256)
         last_mod = keep.tile([P, HID], U8, align_bytes=256)
         last_tgt = keep.tile([P, HID], U8, align_bytes=256)
-        row_vecs = keep.tile([P, COLS], BF16)
+        bias_rows = keep.tile([P, BANK], BF16)
+        b_tgt_rows = keep.tile([P, BANK], BF16)
         unit_rows = keep.tile([P, P], BF16)
-        dt_sb = keep.tile([P, TILES], BF16)
+        dt_sb = keep.tile([P, B_TILES], BF16)
         warm = keep.tile([P, 1], F32)
-        zeros = keep.tile([P, COLS], BF16)
-        nc.vector.memset(zeros[:], 0.0)
-        nc.vector.memset(row_vecs[:], 0.0)
+        nc.vector.memset(bias_rows[:], 0.0)
         nc.vector.memset(warm[:], 0.0)
         nc.vector.memset(planes_mod[:].bitcast(I32), 0)
+        nc.vector.memset(b_tgt_rows[:], 0.0)
         nc.vector.memset(unit_rows[:], 0.0)
         nc.vector.memset(last_mod[:].bitcast(I32), 0)
         nc.vector.memset(planes_tgt[:].bitcast(I32), 0)
         nc.vector.memset(last_tgt[:].bitcast(I32), 0)
 
-        x_sb = keep.tile([P, TILES, IN], BF16)
-        h_sb = keep.tile([P, TILES, HID], BF16)
-        x_view = x.rearrange("(p j) k -> p j k", j=TILES)
-        h_view = h.rearrange("(p j) k -> p j k", j=TILES)
-        out_view = out.rearrange("(p j) n -> p j n", j=TILES)
+        x_sb = keep.tile([P, B_TILES, IN], BF16)
+        h_sb = keep.tile([P, B_TILES, HID], BF16)
+        x_view = x.rearrange("(p j) k -> p j k", j=B_TILES)
+        h_view = h.rearrange("(p j) k -> p j k", j=B_TILES)
+        out_view = out.rearrange("(p j) n -> p j n", j=B_TILES)
 
         w_mod_sb = keep.tile([P, PASSES, HID], U32, align_bytes=256)
         w_tgt_sb = keep.tile([P, PASSES, HID], U32, align_bytes=256)
-
-        def load_h(first, last):
-            nc.sync.dma_start(out=h_sb[:, :, first:last], in_=h_view[:, :, first:last])
 
         def load_scales(scales, planes):
             for quad in range(4):
@@ -89,98 +83,97 @@ def tile_ltccell_kernel(
                     in_=scales[PLANES_PER_TILE, 4 * quad : 4 * quad + 4, :].bitcast(I32),
                 )
 
-        def load_words(words, w_sb, first, width, passes):
-            last = first + width
+        def load_words(words, w_sb, first, last):
             nc.sync.dma_start(
-                out=w_sb[:, passes, first:last].bitcast(I32),
-                in_=words.rearrange("g p n t -> p g (n t)")[:, passes, PACK * first : PACK * last].bitcast(I32),
+                out=w_sb[:, :, first:last].bitcast(I32),
+                in_=words.rearrange("g p n t -> p g (n t)")[:, :, PACK * first : PACK * last].bitcast(I32),
             )
 
-        nc.scalar.dma_start(out=row_vecs[0:BLOCKS, :], in_=bias.rearrange("(r c) -> r c", c=COLS))
+        nc.scalar.dma_start(out=bias_rows[0:4, :], in_=bias.rearrange("(r c) -> r c", c=BANK))
         nc.scalar.activation(out=warm[:], in_=warm[:], func=ACT.Exp)
         nc.sync.dma_start(out=x_sb[:], in_=x_view)
         load_scales(W_mod_scales, planes_mod)
-        load_h(0, K_PASS)
-        load_words(W_mod_words, w_mod_sb, 0, COLS, slice(0, 1))
-        load_h(K_PASS, 2 * K_PASS)
-        load_words(W_mod_words, w_mod_sb, 0, COLS, slice(1, 2))
+        for j in range(B_TILES):
+            nc.sync.dma_start(out=h_sb[:, j, :], in_=h_view[:, j, :])
         load_last_scales(W_mod_scales, last_mod)
-        load_h(2 * K_PASS, 3 * K_PASS)
-        load_words(W_mod_words, w_mod_sb, 0, COLS, slice(2, 3))
-        load_h(3 * K_PASS, 4 * K_PASS)
-        load_words(W_mod_words, w_mod_sb, 0, COLS, slice(3, 5))
+        load_words(W_mod_words, w_mod_sb, 0, 256)
+        load_words(W_mod_words, w_mod_sb, 256, 512)
         load_scales(W_tgt_scales, planes_tgt)
-        load_words(W_tgt_words, w_tgt_sb, 0, COLS, slice(0, 5))
-        for half in range(2):
-            load_words(W_mod_words, w_mod_sb, COLS + COLS // 2 * half, COLS // 2, slice(0, 5))
+        load_words(W_tgt_words, w_tgt_sb, 0, 512)
         load_last_scales(W_tgt_scales, last_tgt)
-        load_words(W_tgt_words, w_tgt_sb, COLS, COLS, slice(0, 5))
-        for block in range(2, BLOCKS):
-            load_words(W_mod_words, w_mod_sb, COLS * block, COLS, slice(0, 5))
-            load_words(W_tgt_words, w_tgt_sb, COLS * block, COLS, slice(0, 5))
+        load_words(W_mod_words, w_mod_sb, 512, 768)
+        load_words(W_mod_words, w_mod_sb, 768, 1024)
+        load_words(W_tgt_words, w_tgt_sb, 512, 1024)
+        for first in (1024, 1536):
+            load_words(W_mod_words, w_mod_sb, first, first + 512)
+            load_words(W_tgt_words, w_tgt_sb, first, first + 512)
 
         ident_f32 = keep.tile([P, P], F32)
         make_identity(nc, ident_f32[:])
         ident_bf16 = keep.tile([P, P], BF16)
         nc.vector.tensor_copy(out=ident_bf16[:], in_=ident_f32[:])
-        n_tiles = HID // P
-        nc.gpsimd.dma_start(out=row_vecs[BLOCKS : 2 * BLOCKS, :], in_=b_tgt.rearrange("(r c) -> r c", c=COLS))
-        nc.gpsimd.dma_start(out=unit_rows[0:n_tiles, :], in_=b_mod.rearrange("(r c) -> r c", c=P))
-        nc.gpsimd.dma_start(out=unit_rows[n_tiles : 2 * n_tiles, :], in_=log_tau.rearrange("(r c) -> r c", c=P))
-        nc.gpsimd.dma_start(out=dt_sb[:], in_=time_delta.rearrange("(p j) o -> p (j o)", j=TILES))
+        nc.gpsimd.dma_start(out=b_tgt_rows[0:4, :], in_=b_tgt.rearrange("(r c) -> r c", c=BANK))
+        nc.gpsimd.dma_start(out=unit_rows[0:U_TILES, :], in_=b_mod.rearrange("(r c) -> r c", c=P))
+        nc.gpsimd.dma_start(out=unit_rows[U_TILES : 2 * U_TILES, :], in_=log_tau.rearrange("(r c) -> r c", c=P))
+        nc.gpsimd.dma_start(out=dt_sb[:], in_=time_delta.rearrange("(p j) o -> p (j o)", j=B_TILES))
 
         bias_all = keep.tile([P, HID], BF16)
         b_tgt_all = keep.tile([P, HID], BF16)
 
-        def spread(first_row, target):
-            for pair in range(BLOCKS // 2):
-                spread_ps = flip_psum.tile([P, 2 * COLS], BF16, tag="flip")
+        def spread(rows, target):
+            for pair in range(2):
+                spread_ps = flip_psum.tile([P, 2 * BANK], BF16, tag="flip")
                 for part in range(2):
-                    row = first_row + 2 * pair + part
+                    row = 2 * pair + part
                     nc.tensor.matmul(
-                        spread_ps[:, COLS * part : COLS * (part + 1)],
+                        spread_ps[:, BANK * part : BANK * (part + 1)],
                         lhsT=ident_bf16[:, row : row + 1].to_broadcast([P, P]),
-                        rhs=row_vecs[:],
+                        rhs=rows[:],
                         start=True,
                         stop=True,
                     )
-                nc.scalar.copy(out=target[:, 2 * COLS * pair : 2 * COLS * (pair + 1)], in_=spread_ps[:])
+                nc.scalar.copy(out=target[:, 2 * BANK * pair : 2 * BANK * (pair + 1)], in_=spread_ps[:])
+
+        h_less_bias = keep.tile([P, B_TILES, HID], F32)
+        less_bias_left = [(j, b) for j in range(B_TILES) for b in range(HID // BANK)]
+
+        def less_bias(count):
+            for n in range(min(count, len(less_bias_left))):
+                j, b = less_bias_left.pop(0)
+                cols = slice(BANK * b, BANK * (b + 1))
+                nc.vector.tensor_tensor(
+                    out=h_less_bias[:, j, cols], in0=h_sb[:, j, cols], in1=bias_all[:, cols], op=ALU.subtract
+                )
 
         ct_codes = keep.tile([P, PASSES, BATCH], U32, align_bytes=256)
         ct_scales = keep.tile([P, PASSES, BATCH], U8, align_bytes=256)
 
-        def transpose_pass(g):
-            grouped = stage.tile([P, BATCH * PACK], BF16, align_bytes=64)
-            grouped_words = grouped[:].bitcast(F32).rearrange("p (b u) -> p b u", u=2)
-            for half in range(2):
-                flipped = flip_psum.tile([P, 2, 2 * P], F32, tag="flip")
-                for jj in range(2):
-                    j = 2 * half + jj
-                    if g == 0:
-                        words = x_sb[:, j, :].bitcast(F32)
-                    else:
-                        words = h_sb[:, j, K_PASS * (g - 1) : K_PASS * g].bitcast(F32)
-                    for u in range(2):
-                        nc.tensor.transpose(flipped[:, u, P * jj : P * (jj + 1)], words[:, u : 2 * P : 2], ident_f32[:])
-                source = flipped[:].rearrange("p u b -> p b u")
-                target = grouped_words[:, 2 * P * half : 2 * P * (half + 1), :]
+        def transpose_half(g, half, grouped, engine):
+            flipped = flip_psum.tile([P, 2, 2 * P], F32, tag="flip", name="flip")
+            for jj in range(2):
+                j = 2 * half + jj
+                if g == 0:
+                    words = x_sb[:, j, :].bitcast(F32)
+                else:
+                    words = h_sb[:, j, K_PASS * (g - 1) : K_PASS * g].bitcast(F32)
+                for u in range(2):
+                    nc.tensor.transpose(flipped[:, u, P * jj : P * (jj + 1)], words[:, u : 2 * P : 2], ident_f32[:])
+            source = flipped[:].rearrange("p u b -> p b u")
+            target = grouped[:].bitcast(F32).rearrange("p (b u) -> p b u", u=2)[:, 2 * P * half : 2 * P * (half + 1), :]
+            if engine == "vector":
+                nc.vector.tensor_copy(out=target, in_=source)
+            else:
                 nc.scalar.copy(out=target, in_=source)
-            return grouped
 
         def quantise_pass(g, grouped):
             nc.vector.quantize_mx(out=ct_codes[:, g, :].bitcast(FP8X4), scales=ct_scales[:, g, :], in_=grouped[:])
-
-        def weight_scale(w, g, cols):
-            if g < PLANES_PER_TILE:
-                return (planes_mod, planes_tgt)[w][4 * g : P, cols]
-            return (last_mod, last_tgt)[w][:, cols]
 
         def f_pass(acc, i, g):
             cols = slice(P * i, P * (i + 1))
             nc.tensor.matmul_mx(
                 out=acc[:],
                 lhsT=w_mod_sb[:, g, cols].bitcast(FP8X4),
-                lhsT_scale=weight_scale(0, g, cols),
+                lhsT_scale=planes_mod[4 * g : P, cols] if g < PLANES_PER_TILE else last_mod[:, cols],
                 rhs=ct_codes[:, g, :].bitcast(FP8X4),
                 rhs_scale=ct_scales[:, g, :],
                 start=(g == 0),
@@ -194,30 +187,59 @@ def tile_ltccell_kernel(
                 lhsT=ct_codes[:, g, rows].bitcast(FP8X4),
                 lhsT_scale=ct_scales[:, g, rows],
                 rhs=w_tgt_sb[:, g, cols].bitcast(FP8X4),
-                rhs_scale=weight_scale(1, g, cols),
+                rhs_scale=planes_tgt[4 * g : P, cols] if g < PLANES_PER_TILE else last_tgt[:, cols],
                 start=(g == 0),
                 stop=(g == PASSES - 1),
             )
 
-        tiles = [(r, j) for r in range(len(ROUNDS)) for j in range(TILES)]
-        h_less_bias = keep.tile([P, TILES, HID], F32)
-        less_bias_left = [(block, j) for block in range(BLOCKS) for j in range(TILES)]
+        with tc.tile_pool(name="stage", bufs=1) as stage:
+            grouped = []
+            for g in range(PASSES):
+                grouped.append(stage.tile([P, BATCH * PACK], BF16, align_bytes=256, tag="grouped%d" % g, name="grouped"))
+            spread(bias_rows, bias_all)
+            transpose_half(0, 0, grouped[0], "scalar")
+            transpose_half(0, 1, grouped[0], "vector")
+            spread(b_tgt_rows, b_tgt_all)
+            quantise_pass(0, grouped[0])
+            for g in range(1, PASSES):
+                transpose_half(g, 0, grouped[g], "scalar")
+            less_bias(4)
+            for g in range(1, PASSES):
+                transpose_half(g, 1, grouped[g], "scalar" if g > 1 else "vector")
+                quantise_pass(g, grouped[g])
+        work = ctx.enter_context(tc.tile_pool(name="work", bufs=4))
+
+        unit_ps = flip_psum.tile([P, P], BF16, tag="flip")
+        nc.tensor.transpose(unit_ps[:], unit_rows[:], ident_bf16[:])
+        unit_cols = keep.tile([P, 2 * U_TILES], F32)
+        nc.vector.tensor_copy(out=unit_cols[:], in_=unit_ps[:, 0 : 2 * U_TILES])
+        b_mod_cols = unit_cols[:, 0:U_TILES]
+
+        inv_tau = keep.tile([P, U_TILES], F32)
+        seed = keep.tile([P, U_TILES], F32)
+        slope = keep.tile([P, U_TILES], F32)
+        base = keep.tile([P, U_TILES], F32)
+        neg_dt = keep.tile([P, B_TILES], F32)
+        nc.scalar.activation(out=inv_tau[:], in_=unit_cols[:, U_TILES : 2 * U_TILES], func=ACT.Exp, scale=-1.0)
+        nc.vector.tensor_scalar(out=neg_dt[:], in0=dt_sb[:], scalar1=-1.0, scalar2=None, op0=ALU.mult)
+        nc.vector.tensor_scalar(out=seed[:], in0=inv_tau[:], scalar1=EPS, scalar2=1.0, op0=ALU.mult, op1=ALU.add)
+        nc.vector.reciprocal(out=seed[:], in_=seed[:])
+        nc.vector.tensor_tensor(out=slope[:], in0=seed[:], in1=seed[:], op=ALU.mult)
+        nc.vector.tensor_tensor(out=base[:], in0=seed[:], in1=inv_tau[:], op=ALU.mult)
+        nc.vector.scalar_tensor_tensor(
+            out=base[:], in0=slope[:], scalar=-EPS, in1=base[:], op0=ALU.mult, op1=ALU.add
+        )
+
+        tiles = [(r, j) for r in range(len(ROUNDS)) for j in range(B_TILES)]
         goal, decay, rates, abs_v, flips = {}, {}, {}, {}, {}
 
         def units(r):
             first, width = ROUNDS[r]
             return slice(first, first + width)
 
-        def less_bias():
-            block, j = less_bias_left.pop(0)
-            cols = slice(COLS * block, COLS * (block + 1))
-            nc.vector.tensor_tensor(
-                out=h_less_bias[:, j, cols], in0=h_sb[:, j, cols], in1=bias_all[:, cols], op=ALU.subtract
-            )
-
         def add_b_tgt(n, acc):
             r, j = tiles[n]
-            goal[n] = work.tile([P, ROUNDS[r][1]], F32, tag="goal", bufs=7, name="goal")
+            goal[n] = work.tile([P, ROUNDS[r][1]], F32, tag="goal", bufs=8, name="goal")
             nc.vector.tensor_tensor(out=goal[n][:], in0=acc, in1=b_tgt_all[:, units(r)], op=ALU.add)
 
         def tanh_goal(n):
@@ -254,68 +276,25 @@ def tile_ltccell_kernel(
 
         def rate_of(i):
             rates[i] = work.tile([P, BATCH], F32, tag="rate", bufs=6, name="rate")
-            nc.vector.tensor_scalar(
-                out=rates[i][:], in0=abs_v[i][:], scalar1=slope[:, i : i + 1], scalar2=base[:, i : i + 1],
-                op0=ALU.mult, op1=ALU.add,
-            )
+            if i < VECTOR_RATES:
+                nc.vector.tensor_scalar(
+                    out=rates[i][:], in0=abs_v[i][:], scalar1=slope[:, i : i + 1], scalar2=base[:, i : i + 1],
+                    op0=ALU.mult, op1=ALU.add,
+                )
+            else:
+                nc.scalar.activation(
+                    out=rates[i][:], in_=abs_v[i][:], func=ACT.Identity, scale=slope[:, i : i + 1], bias=base[:, i : i + 1]
+                )
 
         def flip_rates(r):
             first, width = ROUNDS[r]
-            for j in range(TILES):
+            for j in range(B_TILES):
                 flip = flip_psum.tile([P, width], F32, tag="flip", name="flip")
                 for ii in range(width // P):
                     nc.tensor.transpose(
                         flip[:, P * ii : P * (ii + 1)], rates[first // P + ii][:, P * j : P * (j + 1)], ident_f32[:]
                     )
-                flips[TILES * r + j] = flip
-
-        accs = [acc_psum.tile([P, BATCH], F32, tag="acc", name="acc") for i in range(HEAD_TILES)]
-
-        def head_pass(g):
-            for i in range(HEAD_TILES):
-                f_pass(accs[i], i, g)
-
-        idle_ps = flip_psum.tile([P, COLS], F32, tag="flip")
-        for n in range(WARM_UP):
-            nc.tensor.matmul(idle_ps[:], lhsT=zeros[:, 0:P], rhs=zeros[:], start=True, stop=True)
-        grouped = transpose_pass(0)
-        spread(0, bias_all)
-        for g in range(1, PASSES):
-            quantise_pass(g - 1, grouped)
-            grouped = transpose_pass(g)
-            for n in range(3):
-                less_bias()
-            if g == PASSES - 1:
-                spread(BLOCKS, b_tgt_all)
-            head_pass(g - 1)
-        quantise_pass(PASSES - 1, grouped)
-
-        unit_ps = flip_psum.tile([P, P], BF16, tag="flip")
-        nc.tensor.transpose(unit_ps[:], unit_rows[:], ident_bf16[:])
-        unit_cols = keep.tile([P, 2 * n_tiles], F32)
-        nc.vector.tensor_copy(out=unit_cols[:], in_=unit_ps[:, 0 : 2 * n_tiles])
-        b_mod_cols = unit_cols[:, 0:n_tiles]
-
-        inv_tau = keep.tile([P, n_tiles], F32)
-        seed = keep.tile([P, n_tiles], F32)
-        slope = keep.tile([P, n_tiles], F32)
-        base = keep.tile([P, n_tiles], F32)
-        neg_dt = keep.tile([P, TILES], F32)
-        nc.scalar.activation(out=inv_tau[:], in_=unit_cols[:, n_tiles : 2 * n_tiles], func=ACT.Exp, scale=-1.0)
-        nc.vector.tensor_scalar(out=neg_dt[:], in0=dt_sb[:], scalar1=-1.0, scalar2=None, op0=ALU.mult)
-        nc.vector.tensor_scalar(out=seed[:], in0=inv_tau[:], scalar1=EPS, scalar2=1.0, op0=ALU.mult, op1=ALU.add)
-        nc.vector.reciprocal(out=seed[:], in_=seed[:])
-        nc.vector.tensor_tensor(out=slope[:], in0=seed[:], in1=seed[:], op=ALU.mult)
-        nc.vector.tensor_tensor(out=base[:], in0=seed[:], in1=inv_tau[:], op=ALU.mult)
-        nc.vector.scalar_tensor_tensor(
-            out=base[:], in0=slope[:], scalar=-EPS, in1=base[:], op0=ALU.mult, op1=ALU.add
-        )
-        head_pass(PASSES - 1)
-
-        for i in range(HEAD_TILES):
-            abs_of(i, accs[i])
-        while less_bias_left:
-            less_bias()
+                flips[B_TILES * r + j] = flip
 
         def f_group(i):
             acc = acc_psum.tile([P, BATCH], F32, tag="acc", name="acc")
@@ -325,48 +304,60 @@ def tile_ltccell_kernel(
 
         def a_group(n):
             r, j = tiles[n]
-            acc = acc_psum.tile([P, COLS], F32, tag="acc", name="acc")
+            acc = acc_psum.tile([P, BANK], F32, tag="acc", name="acc")
             part = acc[:, 0 : ROUNDS[r][1]]
             for g in range(PASSES):
                 a_pass(part, units(r), j, g)
             return part
 
-        f_after = {n: n + HEAD_TILES for n in range(10)}
-        f_after[11] = 14
-        f_after[13] = 15
+        accs = [acc_psum.tile([P, BATCH], F32, tag="acc", name="acc") for i in range(HEAD_TILES)]
+        for g in range(PASSES):
+            for i in range(HEAD_TILES):
+                f_pass(accs[i], i, g)
+        less_bias(7)
+        for i in range(HEAD_TILES):
+            abs_of(i, accs[i])
+
+        f_after = {n: [n + HEAD_TILES] for n in range(9)}
+        f_after[10] = [13]
+        f_after[11] = [14]
+        f_after[13] = [15]
         flip_after = {1: 0, 5: 1, 9: 2, 13: 3, 17: 4}
         f_waiting = list(range(HEAD_TILES))
         to_decay, decayed = [], []
         for n in range(len(tiles)):
             acc = a_group(n)
+            for i in f_waiting:
+                tanh_f(i)
             for m in to_decay[0:2]:
                 decay_of(m)
             decayed += to_decay[0:2]
             to_decay = to_decay[2:]
             for i in f_waiting:
-                tanh_f(i)
+                if i >= VECTOR_RATES:
+                    rate_of(i)
             add_b_tgt(n, acc)
             tanh_goal(n)
-            count = 2 if n > 13 else 1
-            blends = [m for m in decayed[0:count] if m < n - 1]
+            for i in f_waiting:
+                if i < VECTOR_RATES:
+                    rate_of(i)
+            blends = [m for m in decayed[0:2] if m < n - 1]
             decayed = decayed[len(blends) :]
             for m in blends:
                 shrink(m)
             if n > 0:
                 pull(n - 1)
-            for i in f_waiting:
-                rate_of(i)
             for m in blends:
                 finish(m)
+            less_bias(1)
             f_waiting = []
-            if n in f_after:
-                i = f_after[n]
+            for i in f_after.get(n, []):
                 abs_of(i, f_group(i))
-                f_waiting = [i]
+                f_waiting.append(i)
             if n in flip_after:
                 r = flip_after[n]
                 flip_rates(r)
-                to_decay = to_decay + list(range(TILES * r, TILES * (r + 1)))
+                to_decay = to_decay + list(range(B_TILES * r, B_TILES * (r + 1)))
         pull(len(tiles) - 1)
         for m in to_decay:
             decay_of(m)

@@ -26,6 +26,7 @@ BANK = 512
 ROUNDS = ((0, 512), (512, 512), (1024, 512), (1536, 256), (1792, 256))
 HEAD_TILES = 4
 PLANES_PER_TILE = 4
+LAST_COLS = HID // PLANES_PER_TILE
 VECTOR_RATES = 10
 EPS = 1e-6
 
@@ -44,8 +45,8 @@ def tile_ltccell_kernel(
 
         planes_mod = keep.tile([P, HID], U8, align_bytes=256)
         planes_tgt = keep.tile([P, HID], U8, align_bytes=256)
-        last_mod = keep.tile([P, HID], U8, align_bytes=256)
-        last_tgt = keep.tile([P, HID], U8, align_bytes=256)
+        last_mod = keep.tile([P, LAST_COLS], U8, align_bytes=256)
+        last_tgt = keep.tile([P, LAST_COLS], U8, align_bytes=256)
         bias_rows = keep.tile([P, BANK], BF16)
         b_tgt_rows = keep.tile([P, BANK], BF16)
         unit_rows = keep.tile([P, P], BF16)
@@ -76,11 +77,12 @@ def tile_ltccell_kernel(
                     in_=scales[0:PLANES_PER_TILE, 4 * quad : 4 * quad + 4, :].bitcast(I32),
                 )
 
-        def load_last_scales(scales, plane):
+        def load_last_scales(scales, planes):
             for quad in range(4):
+                rows = scales[PLANES_PER_TILE, 4 * quad : 4 * quad + 4, :].bitcast(I32)
                 nc.sync.dma_start(
-                    out=plane[32 * quad : 32 * quad + 4, :].bitcast(I32),
-                    in_=scales[PLANES_PER_TILE, 4 * quad : 4 * quad + 4, :].bitcast(I32),
+                    out=planes[32 * quad : 32 * quad + 16, :].bitcast(I32),
+                    in_=rows.rearrange("r (x n) -> x r n", x=PLANES_PER_TILE),
                 )
 
         def load_words(words, w_sb, first, last):
@@ -168,12 +170,18 @@ def tile_ltccell_kernel(
         def quantise_pass(g, grouped):
             nc.vector.quantize_mx(out=ct_codes[:, g, :].bitcast(FP8X4), scales=ct_scales[:, g, :], in_=grouped[:])
 
+        def weight_scale(planes, last, g, cols):
+            if g < PLANES_PER_TILE:
+                return planes[4 * g : P, cols]
+            part = cols.start // LAST_COLS
+            return last[4 * part : P, cols.start - LAST_COLS * part : cols.stop - LAST_COLS * part]
+
         def f_pass(acc, i, g):
             cols = slice(P * i, P * (i + 1))
             nc.tensor.matmul_mx(
                 out=acc[:],
                 lhsT=w_mod_sb[:, g, cols].bitcast(FP8X4),
-                lhsT_scale=planes_mod[4 * g : P, cols] if g < PLANES_PER_TILE else last_mod[:, cols],
+                lhsT_scale=weight_scale(planes_mod, last_mod, g, cols),
                 rhs=ct_codes[:, g, :].bitcast(FP8X4),
                 rhs_scale=ct_scales[:, g, :],
                 start=(g == 0),
@@ -187,7 +195,7 @@ def tile_ltccell_kernel(
                 lhsT=ct_codes[:, g, rows].bitcast(FP8X4),
                 lhsT_scale=ct_scales[:, g, rows],
                 rhs=w_tgt_sb[:, g, cols].bitcast(FP8X4),
-                rhs_scale=planes_tgt[4 * g : P, cols] if g < PLANES_PER_TILE else last_tgt[:, cols],
+                rhs_scale=weight_scale(planes_tgt, last_tgt, g, cols),
                 start=(g == 0),
                 stop=(g == PASSES - 1),
             )

@@ -23,6 +23,7 @@ PASSES = K // K_PASS
 B_TILES = BATCH // P
 U_TILES = HID // P
 BANK = 512
+LOAD_COLS = 512
 ROUNDS = ((0, 512), (512, 512), (1024, 512), (1536, 256), (1792, 256))
 HEAD_TILES = 4
 PLANES_PER_TILE = 4
@@ -85,10 +86,11 @@ def tile_ltccell_kernel(
                     in_=rows.rearrange("r (x n) -> x r n", x=PLANES_PER_TILE),
                 )
 
-        def load_words(words, w_sb, first, last):
+        def load_words(words, w_sb, first, passes, width=LOAD_COLS):
+            last = first + width
             nc.sync.dma_start(
-                out=w_sb[:, :, first:last].bitcast(I32),
-                in_=words.rearrange("g p n t -> p g (n t)")[:, :, PACK * first : PACK * last].bitcast(I32),
+                out=w_sb[:, passes, first:last].bitcast(I32),
+                in_=words.rearrange("g p n t -> p g (n t)")[:, passes, PACK * first : PACK * last].bitcast(I32),
             )
 
         nc.scalar.dma_start(out=bias_rows[0:4, :], in_=bias.rearrange("(r c) -> r c", c=BANK))
@@ -98,17 +100,17 @@ def tile_ltccell_kernel(
         for j in range(B_TILES):
             nc.sync.dma_start(out=h_sb[:, j, :], in_=h_view[:, j, :])
         load_last_scales(W_mod_scales, last_mod)
-        load_words(W_mod_words, w_mod_sb, 0, 256)
-        load_words(W_mod_words, w_mod_sb, 256, 512)
+        load_words(W_mod_words, w_mod_sb, 0, slice(0, 2))
+        load_words(W_mod_words, w_mod_sb, 0, slice(2, 5))
         load_scales(W_tgt_scales, planes_tgt)
-        load_words(W_tgt_words, w_tgt_sb, 0, 512)
+        load_words(W_tgt_words, w_tgt_sb, 0, slice(0, 5))
         load_last_scales(W_tgt_scales, last_tgt)
-        load_words(W_mod_words, w_mod_sb, 512, 768)
-        load_words(W_mod_words, w_mod_sb, 768, 1024)
-        load_words(W_tgt_words, w_tgt_sb, 512, 1024)
+        for block in range(2):
+            load_words(W_mod_words, w_mod_sb, 512 + 256 * block, slice(0, 5), 256)
+        load_words(W_tgt_words, w_tgt_sb, 512, slice(0, 5))
         for first in (1024, 1536):
-            load_words(W_mod_words, w_mod_sb, first, first + 512)
-            load_words(W_tgt_words, w_tgt_sb, first, first + 512)
+            load_words(W_mod_words, w_mod_sb, first, slice(0, 5))
+            load_words(W_tgt_words, w_tgt_sb, first, slice(0, 5))
 
         ident_f32 = keep.tile([P, P], F32)
         make_identity(nc, ident_f32[:])
@@ -200,6 +202,29 @@ def tile_ltccell_kernel(
                 stop=(g == PASSES - 1),
             )
 
+        inv_tau = keep.tile([P, U_TILES], F32)
+        seed = keep.tile([P, U_TILES], F32)
+        slope = keep.tile([P, U_TILES], F32)
+        base = keep.tile([P, U_TILES], F32)
+        neg_dt = keep.tile([P, B_TILES], F32)
+        unit_cols = keep.tile([P, 2 * U_TILES], F32)
+        b_mod_cols = unit_cols[:, 0:U_TILES]
+
+        def unit_constants():
+            unit_ps = flip_psum.tile([P, 2 * U_TILES], F32, tag="flip")
+            nc.tensor.matmul(unit_ps[:], lhsT=unit_rows[:], rhs=ident_bf16[:, 0 : 2 * U_TILES], start=True, stop=True)
+            nc.vector.tensor_copy(out=unit_cols[:], in_=unit_ps[:])
+
+            nc.scalar.activation(out=inv_tau[:], in_=unit_cols[:, U_TILES : 2 * U_TILES], func=ACT.Exp, scale=-1.0)
+            nc.vector.tensor_scalar(out=neg_dt[:], in0=dt_sb[:], scalar1=-1.0, scalar2=None, op0=ALU.mult)
+            nc.vector.tensor_scalar(out=seed[:], in0=inv_tau[:], scalar1=EPS, scalar2=1.0, op0=ALU.mult, op1=ALU.add)
+            nc.vector.reciprocal(out=seed[:], in_=seed[:])
+            nc.vector.tensor_tensor(out=slope[:], in0=seed[:], in1=seed[:], op=ALU.mult)
+            nc.vector.tensor_tensor(out=base[:], in0=seed[:], in1=inv_tau[:], op=ALU.mult)
+            nc.vector.scalar_tensor_tensor(
+                out=base[:], in0=slope[:], scalar=-EPS, in1=base[:], op0=ALU.mult, op1=ALU.add
+            )
+
         with tc.tile_pool(name="stage", bufs=1) as stage:
             grouped = []
             for g in range(PASSES):
@@ -215,28 +240,8 @@ def tile_ltccell_kernel(
             for g in range(1, PASSES):
                 transpose_half(g, 1, grouped[g], "scalar" if g > 1 else "vector")
                 quantise_pass(g, grouped[g])
+        unit_constants()
         work = ctx.enter_context(tc.tile_pool(name="work", bufs=4))
-
-        unit_ps = flip_psum.tile([P, P], BF16, tag="flip")
-        nc.tensor.transpose(unit_ps[:], unit_rows[:], ident_bf16[:])
-        unit_cols = keep.tile([P, 2 * U_TILES], F32)
-        nc.vector.tensor_copy(out=unit_cols[:], in_=unit_ps[:, 0 : 2 * U_TILES])
-        b_mod_cols = unit_cols[:, 0:U_TILES]
-
-        inv_tau = keep.tile([P, U_TILES], F32)
-        seed = keep.tile([P, U_TILES], F32)
-        slope = keep.tile([P, U_TILES], F32)
-        base = keep.tile([P, U_TILES], F32)
-        neg_dt = keep.tile([P, B_TILES], F32)
-        nc.scalar.activation(out=inv_tau[:], in_=unit_cols[:, U_TILES : 2 * U_TILES], func=ACT.Exp, scale=-1.0)
-        nc.vector.tensor_scalar(out=neg_dt[:], in0=dt_sb[:], scalar1=-1.0, scalar2=None, op0=ALU.mult)
-        nc.vector.tensor_scalar(out=seed[:], in0=inv_tau[:], scalar1=EPS, scalar2=1.0, op0=ALU.mult, op1=ALU.add)
-        nc.vector.reciprocal(out=seed[:], in_=seed[:])
-        nc.vector.tensor_tensor(out=slope[:], in0=seed[:], in1=seed[:], op=ALU.mult)
-        nc.vector.tensor_tensor(out=base[:], in0=seed[:], in1=inv_tau[:], op=ALU.mult)
-        nc.vector.scalar_tensor_tensor(
-            out=base[:], in0=slope[:], scalar=-EPS, in1=base[:], op0=ALU.mult, op1=ALU.add
-        )
 
         tiles = [(r, j) for r in range(len(ROUNDS)) for j in range(B_TILES)]
         goal, decay, rates, abs_v, flips = {}, {}, {}, {}, {}
@@ -327,6 +332,10 @@ def tile_ltccell_kernel(
             abs_of(i, accs[i])
 
         f_after = {n: [n + HEAD_TILES] for n in range(9)}
+        f_after[0] = []
+        f_after[1] = [4]
+        f_after[2] = [5]
+        f_after[3] = [6, 7]
         f_after[10] = [13]
         f_after[11] = [14]
         f_after[13] = [15]

@@ -28,7 +28,7 @@ ROUNDS = ((0, 512), (512, 512), (1024, 512), (1536, 256), (1792, 256))
 HEAD_TILES = 4
 PLANES_PER_TILE = 4
 LAST_COLS = HID // PLANES_PER_TILE
-VECTOR_RATES = 10
+VECTOR_RATES = 12
 EPS = 1e-6
 
 FLOPS = 2 * 2 * BATCH * K * HID
@@ -103,14 +103,14 @@ def tile_ltccell_kernel(
         load_words(W_mod_words, w_mod_sb, 0, slice(0, 2))
         load_words(W_mod_words, w_mod_sb, 0, slice(2, 5))
         load_scales(W_tgt_scales, planes_tgt)
-        load_words(W_tgt_words, w_tgt_sb, 0, slice(0, 5))
+        load_words(W_tgt_words, w_tgt_sb, 0, slice(0, 2))
+        load_words(W_tgt_words, w_tgt_sb, 0, slice(2, 5))
         load_last_scales(W_tgt_scales, last_tgt)
         for block in range(2):
             load_words(W_mod_words, w_mod_sb, 512 + 256 * block, slice(0, 5), 256)
         load_words(W_tgt_words, w_tgt_sb, 512, slice(0, 5))
-        for first in (1024, 1536):
-            load_words(W_mod_words, w_mod_sb, first, slice(0, 5))
-            load_words(W_tgt_words, w_tgt_sb, first, slice(0, 5))
+        load_words(W_mod_words, w_mod_sb, 1024, slice(0, 5))
+        load_words(W_tgt_words, w_tgt_sb, 1024, slice(0, 5))
 
         ident_f32 = keep.tile([P, P], F32)
         make_identity(nc, ident_f32[:])
@@ -152,17 +152,24 @@ def tile_ltccell_kernel(
         ct_codes = keep.tile([P, PASSES, BATCH], U32, align_bytes=256)
         ct_scales = keep.tile([P, PASSES, BATCH], U8, align_bytes=256)
 
-        def transpose_half(g, half, grouped, engine):
-            flipped = flip_psum.tile([P, 2, 2 * P], F32, tag="flip", name="flip")
+        def transpose_halves(passes, half):
+            pool, tag = (acc_psum, "acc") if half == 0 and 1 in passes else (flip_psum, "flip")
+            banks = {g: pool.tile([P, 2, 2 * P], F32, tag=tag, name="flip") for g in passes}
             for jj in range(2):
                 j = 2 * half + jj
-                if g == 0:
-                    words = x_sb[:, j, :].bitcast(F32)
-                else:
-                    words = h_sb[:, j, K_PASS * (g - 1) : K_PASS * g].bitcast(F32)
-                for u in range(2):
-                    nc.tensor.transpose(flipped[:, u, P * jj : P * (jj + 1)], words[:, u : 2 * P : 2], ident_f32[:])
-            source = flipped[:].rearrange("p u b -> p b u")
+                for g in passes:
+                    if g == 0:
+                        words = x_sb[:, j, :].bitcast(F32)
+                    else:
+                        words = h_sb[:, j, K_PASS * (g - 1) : K_PASS * g].bitcast(F32)
+                    for u in range(2):
+                        nc.tensor.transpose(
+                            banks[g][:, u, P * jj : P * (jj + 1)], words[:, u : 2 * P : 2], ident_f32[:]
+                        )
+            return banks
+
+        def regroup(bank, half, grouped, engine):
+            source = bank[:].rearrange("p u b -> p b u")
             target = grouped[:].bitcast(F32).rearrange("p (b u) -> p b u", u=2)[:, 2 * P * half : 2 * P * (half + 1), :]
             if engine == "vector":
                 nc.vector.tensor_copy(out=target, in_=source)
@@ -210,11 +217,12 @@ def tile_ltccell_kernel(
         unit_cols = keep.tile([P, 2 * U_TILES], F32)
         b_mod_cols = unit_cols[:, 0:U_TILES]
 
-        def unit_constants():
+        def unit_columns():
             unit_ps = flip_psum.tile([P, 2 * U_TILES], F32, tag="flip")
             nc.tensor.matmul(unit_ps[:], lhsT=unit_rows[:], rhs=ident_bf16[:, 0 : 2 * U_TILES], start=True, stop=True)
             nc.vector.tensor_copy(out=unit_cols[:], in_=unit_ps[:])
 
+        def unit_constants():
             nc.scalar.activation(out=inv_tau[:], in_=unit_cols[:, U_TILES : 2 * U_TILES], func=ACT.Exp, scale=-1.0)
             nc.vector.tensor_scalar(out=neg_dt[:], in0=dt_sb[:], scalar1=-1.0, scalar2=None, op0=ALU.mult)
             nc.vector.tensor_scalar(out=seed[:], in0=inv_tau[:], scalar1=EPS, scalar2=1.0, op0=ALU.mult, op1=ALU.add)
@@ -230,15 +238,19 @@ def tile_ltccell_kernel(
             for g in range(PASSES):
                 grouped.append(stage.tile([P, BATCH * PACK], BF16, align_bytes=256, tag="grouped%d" % g, name="grouped"))
             spread(bias_rows, bias_all)
-            transpose_half(0, 0, grouped[0], "scalar")
-            transpose_half(0, 1, grouped[0], "vector")
+            for half in range(2):
+                regroup(transpose_halves([0], half)[0], half, grouped[0], "vector" if half else "scalar")
             spread(b_tgt_rows, b_tgt_all)
             quantise_pass(0, grouped[0])
-            for g in range(1, PASSES):
-                transpose_half(g, 0, grouped[g], "scalar")
+            h_passes = list(range(1, PASSES))
+            banks = transpose_halves(h_passes, 0)
+            unit_columns()
+            for g in h_passes:
+                regroup(banks[g], 0, grouped[g], "scalar")
             less_bias(4)
-            for g in range(1, PASSES):
-                transpose_half(g, 1, grouped[g], "scalar" if g > 1 else "vector")
+            banks = transpose_halves(h_passes, 1)
+            for g in h_passes:
+                regroup(banks[g], 1, grouped[g], "scalar" if g > 1 else "vector")
                 quantise_pass(g, grouped[g])
         unit_constants()
         work = ctx.enter_context(tc.tile_pool(name="work", bufs=4))
@@ -317,7 +329,8 @@ def tile_ltccell_kernel(
 
         def a_group(n):
             r, j = tiles[n]
-            acc = acc_psum.tile([P, BANK], F32, tag="acc", name="acc")
+            pool, tag = (flip_psum, "flip") if n < 2 else (acc_psum, "acc")
+            acc = pool.tile([P, BANK], F32, tag=tag, name="acc")
             part = acc[:, 0 : ROUNDS[r][1]]
             for g in range(PASSES):
                 a_pass(part, units(r), j, g)
@@ -339,9 +352,10 @@ def tile_ltccell_kernel(
         f_after[10] = [13]
         f_after[11] = [14]
         f_after[13] = [15]
-        flip_after = {1: 0, 5: 1, 9: 2, 13: 3, 17: 4}
+        flip_after = {2: 0, 5: 1, 9: 2, 13: 3, 17: 4}
         f_waiting = list(range(HEAD_TILES))
         to_decay, decayed = [], []
+        late_loads = {4: (W_mod_words, w_mod_sb, 1536), 6: (W_tgt_words, w_tgt_sb, 1536)}
         for n in range(len(tiles)):
             acc = a_group(n)
             for i in f_waiting:
@@ -367,6 +381,8 @@ def tile_ltccell_kernel(
             for m in blends:
                 finish(m)
             less_bias(1)
+            if n in late_loads:
+                load_words(*late_loads[n], slice(0, 5))
             f_waiting = []
             for i in f_after.get(n, []):
                 abs_of(i, f_group(i))

@@ -71,11 +71,12 @@ def tile_ltccell_kernel(
         w_mod_sb = keep.tile([P, PASSES, HID], U32, align_bytes=256)
         w_tgt_sb = keep.tile([P, PASSES, HID], U32, align_bytes=256)
 
-        def load_scales(scales, planes):
+        def load_scales(scales, planes, first, last):
+            cols = slice(first // 4, last // 4)
             for quad in range(4):
                 nc.sync.dma_start(
-                    out=planes[32 * quad : 32 * quad + 16, :].bitcast(I32),
-                    in_=scales[0:PLANES_PER_TILE, 4 * quad : 4 * quad + 4, :].bitcast(I32),
+                    out=planes[32 * quad : 32 * quad + 16, :].bitcast(I32)[:, cols],
+                    in_=scales[0:PLANES_PER_TILE, 4 * quad : 4 * quad + 4, :].bitcast(I32)[:, :, cols],
                 )
 
         def load_last_scales(scales, planes):
@@ -96,18 +97,20 @@ def tile_ltccell_kernel(
         nc.scalar.dma_start(out=bias_rows[0:4, :], in_=bias.rearrange("(r c) -> r c", c=BANK))
         nc.scalar.activation(out=warm[:], in_=warm[:], func=ACT.Exp)
         nc.sync.dma_start(out=x_sb[:], in_=x_view)
-        load_scales(W_mod_scales, planes_mod)
+        load_scales(W_mod_scales, planes_mod, 0, LOAD_COLS)
         for j in range(B_TILES):
             nc.sync.dma_start(out=h_sb[:, j, :], in_=h_view[:, j, :])
         load_last_scales(W_mod_scales, last_mod)
         load_words(W_mod_words, w_mod_sb, 0, slice(0, 2))
         load_words(W_mod_words, w_mod_sb, 0, slice(2, 5))
-        load_scales(W_tgt_scales, planes_tgt)
+        load_scales(W_tgt_scales, planes_tgt, 0, LOAD_COLS)
         load_words(W_tgt_words, w_tgt_sb, 0, slice(0, 2))
-        load_words(W_tgt_words, w_tgt_sb, 0, slice(2, 5))
         load_last_scales(W_tgt_scales, last_tgt)
+        load_words(W_tgt_words, w_tgt_sb, 0, slice(2, 5))
+        load_scales(W_mod_scales, planes_mod, LOAD_COLS, HID)
         for block in range(2):
             load_words(W_mod_words, w_mod_sb, 512 + 256 * block, slice(0, 5), 256)
+        load_scales(W_tgt_scales, planes_tgt, LOAD_COLS, HID)
         load_words(W_tgt_words, w_tgt_sb, 512, slice(0, 5))
         load_words(W_mod_words, w_mod_sb, 1024, slice(0, 5))
         load_words(W_tgt_words, w_tgt_sb, 1024, slice(0, 5))
@@ -220,7 +223,7 @@ def tile_ltccell_kernel(
         def unit_columns():
             unit_ps = flip_psum.tile([P, 2 * U_TILES], F32, tag="flip")
             nc.tensor.matmul(unit_ps[:], lhsT=unit_rows[:], rhs=ident_bf16[:, 0 : 2 * U_TILES], start=True, stop=True)
-            nc.vector.tensor_copy(out=unit_cols[:], in_=unit_ps[:])
+            return unit_ps
 
         def unit_constants():
             nc.scalar.activation(out=inv_tau[:], in_=unit_cols[:, U_TILES : 2 * U_TILES], func=ACT.Exp, scale=-1.0)
@@ -244,10 +247,12 @@ def tile_ltccell_kernel(
             quantise_pass(0, grouped[0])
             h_passes = list(range(1, PASSES))
             banks = transpose_halves(h_passes, 0)
-            unit_columns()
+            less_bias(6)
+            unit_ps = unit_columns()
             for g in h_passes:
                 regroup(banks[g], 0, grouped[g], "scalar")
-            less_bias(4)
+                if g == 2:
+                    nc.scalar.copy(out=unit_cols[:], in_=unit_ps[:])
             banks = transpose_halves(h_passes, 1)
             for g in h_passes:
                 regroup(banks[g], 1, grouped[g], "scalar" if g > 1 else "vector")
@@ -340,18 +345,11 @@ def tile_ltccell_kernel(
         for g in range(PASSES):
             for i in range(HEAD_TILES):
                 f_pass(accs[i], i, g)
-        less_bias(7)
+        less_bias(10)
         for i in range(HEAD_TILES):
             abs_of(i, accs[i])
 
-        f_after = {n: [n + HEAD_TILES] for n in range(9)}
-        f_after[0] = []
-        f_after[1] = [4]
-        f_after[2] = [5]
-        f_after[3] = [6, 7]
-        f_after[10] = [13]
-        f_after[11] = [14]
-        f_after[13] = [15]
+        f_after = {2: [4, 5], 3: [6, 7], 4: [8], 5: [9], 6: [10], 7: [11], 8: [12], 10: [13], 11: [14], 13: [15]}
         flip_after = {2: 0, 5: 1, 9: 2, 13: 3, 17: 4}
         f_waiting = list(range(HEAD_TILES))
         to_decay, decayed = [], []

from contextlib import ExitStack

import concourse.mybir as mybir
from concourse.masks import make_identity

F32 = mybir.dt.float32
BF16 = mybir.dt.bfloat16
I32 = mybir.dt.int32
U32 = mybir.dt.uint32
U8 = mybir.dt.uint8
FP8X4 = mybir.dt.float8_e4m3fn_x4
ACT = mybir.ActivationFunctionType
ALU = mybir.AluOpType

P = 128
PACK = 4
K_PASS = P * PACK
BATCH = 512
IN = 512
HID = 2048
K = IN + HID
PASSES = K // K_PASS
B_TILES = BATCH // P
U_TILES = HID // P
BANK = 512
LOAD_COLS = 512
ROUNDS = ((0, 512), (512, 512), (1024, 512), (1536, 256), (1792, 256))
HEAD_TILES = 4
PLANES_PER_TILE = 4
LAST_COLS = HID // PLANES_PER_TILE
VECTOR_RATES = 12
EPS = 1e-6

FLOPS = 2 * 2 * BATCH * K * HID


def tile_ltccell_kernel(
    tc, x, h, time_delta, W_mod_words, W_mod_scales, b_mod, W_tgt_words, W_tgt_scales, b_tgt, log_tau, bias, out
):
    nc = tc.nc
    with ExitStack() as ctx:
        keep = ctx.enter_context(tc.tile_pool(name="keep", bufs=1))
        acc_psum = ctx.enter_context(tc.psum_pool(name="acc_psum", bufs=4))
        flip_psum = ctx.enter_context(tc.psum_pool(name="flip_psum", bufs=4))
        ctx.enter_context(tc.manual_schedule())

        planes_mod = keep.tile([P, HID], U8, align_bytes=256)
        planes_tgt = keep.tile([P, HID], U8, align_bytes=256)
        last_mod = keep.tile([P, LAST_COLS], U8, align_bytes=256)
        last_tgt = keep.tile([P, LAST_COLS], U8, align_bytes=256)
        bias_rows = keep.tile([P, BANK], BF16)
        b_tgt_rows = keep.tile([P, BANK], BF16)
        unit_rows = keep.tile([P, P], BF16)
        dt_sb = keep.tile([P, B_TILES], BF16)
        warm = keep.tile([P, 1], F32)
        nc.vector.memset(bias_rows[:], 0.0)
        nc.vector.memset(warm[:], 0.0)
        nc.vector.memset(planes_mod[:].bitcast(I32), 0)
        nc.vector.memset(b_tgt_rows[:], 0.0)
        nc.vector.memset(unit_rows[:], 0.0)
        nc.vector.memset(last_mod[:].bitcast(I32), 0)
        nc.vector.memset(planes_tgt[:].bitcast(I32), 0)
        nc.vector.memset(last_tgt[:].bitcast(I32), 0)

        x_sb = keep.tile([P, B_TILES, IN], BF16)
        h_sb = keep.tile([P, B_TILES, HID], BF16)
        x_view = x.rearrange("(p j) k -> p j k", j=B_TILES)
        h_view = h.rearrange("(p j) k -> p j k", j=B_TILES)
        out_view = out.rearrange("(p j) n -> p j n", j=B_TILES)

        w_mod_sb = keep.tile([P, PASSES, HID], U32, align_bytes=256)
        w_tgt_sb = keep.tile([P, PASSES, HID], U32, align_bytes=256)

        def load_scales(scales, planes, first, last):
            cols = slice(first // 4, last // 4)
            for quad in range(4):
                nc.sync.dma_start(
                    out=planes[32 * quad : 32 * quad + 16, :].bitcast(I32)[:, cols],
                    in_=scales[0:PLANES_PER_TILE, 4 * quad : 4 * quad + 4, :].bitcast(I32)[:, :, cols],
                )

        def load_last_scales(scales, planes):
            for quad in range(4):
                rows = scales[PLANES_PER_TILE, 4 * quad : 4 * quad + 4, :].bitcast(I32)
                nc.sync.dma_start(
                    out=planes[32 * quad : 32 * quad + 16, :].bitcast(I32),
                    in_=rows.rearrange("r (x n) -> x r n", x=PLANES_PER_TILE),
                )

        def load_words(words, w_sb, first, passes, width=LOAD_COLS):
            last = first + width
            nc.sync.dma_start(
                out=w_sb[:, passes, first:last].bitcast(I32),
                in_=words.rearrange("g p n t -> p g (n t)")[:, passes, PACK * first : PACK * last].bitcast(I32),
            )

        nc.scalar.dma_start(out=bias_rows[0:4, :], in_=bias.rearrange("(r c) -> r c", c=BANK))
        nc.scalar.activation(out=warm[:], in_=warm[:], func=ACT.Exp)
        nc.sync.dma_start(out=x_sb[:], in_=x_view)
        load_scales(W_mod_scales, planes_mod, 0, LOAD_COLS)
        for j in range(B_TILES):
            nc.sync.dma_start(out=h_sb[:, j, :], in_=h_view[:, j, :])
        load_last_scales(W_mod_scales, last_mod)
        load_words(W_mod_words, w_mod_sb, 0, slice(0, 2))
        load_words(W_mod_words, w_mod_sb, 0, slice(2, 5))
        load_scales(W_tgt_scales, planes_tgt, 0, LOAD_COLS)
        load_words(W_tgt_words, w_tgt_sb, 0, slice(0, 2))
        load_last_scales(W_tgt_scales, last_tgt)
        load_words(W_tgt_words, w_tgt_sb, 0, slice(2, 5))
        load_scales(W_mod_scales, planes_mod, LOAD_COLS, HID)
        for block in range(2):
            load_words(W_mod_words, w_mod_sb, 512 + 256 * block, slice(0, 5), 256)
        load_scales(W_tgt_scales, planes_tgt, LOAD_COLS, HID)
        load_words(W_tgt_words, w_tgt_sb, 512, slice(0, 5))
        load_words(W_mod_words, w_mod_sb, 1024, slice(0, 5))
        load_words(W_tgt_words, w_tgt_sb, 1024, slice(0, 5))

        ident_f32 = keep.tile([P, P], F32)
        make_identity(nc, ident_f32[:])
        ident_bf16 = keep.tile([P, P], BF16)
        nc.vector.tensor_copy(out=ident_bf16[:], in_=ident_f32[:])
        nc.gpsimd.dma_start(out=b_tgt_rows[0:4, :], in_=b_tgt.rearrange("(r c) -> r c", c=BANK))
        nc.gpsimd.dma_start(out=unit_rows[0:U_TILES, :], in_=b_mod.rearrange("(r c) -> r c", c=P))
        nc.gpsimd.dma_start(out=unit_rows[U_TILES : 2 * U_TILES, :], in_=log_tau.rearrange("(r c) -> r c", c=P))
        nc.gpsimd.dma_start(out=dt_sb[:], in_=time_delta.rearrange("(p j) o -> p (j o)", j=B_TILES))

        bias_all = keep.tile([P, HID], BF16)
        b_tgt_all = keep.tile([P, HID], BF16)

        def spread(rows, target):
            for pair in range(2):
                spread_ps = flip_psum.tile([P, 2 * BANK], BF16, tag="flip")
                for part in range(2):
                    row = 2 * pair + part
                    nc.tensor.matmul(
                        spread_ps[:, BANK * part : BANK * (part + 1)],
                        lhsT=ident_bf16[:, row : row + 1].to_broadcast([P, P]),
                        rhs=rows[:],
                        start=True,
                        stop=True,
                    )
                nc.scalar.copy(out=target[:, 2 * BANK * pair : 2 * BANK * (pair + 1)], in_=spread_ps[:])

        h_less_bias = keep.tile([P, B_TILES, HID], F32)
        less_bias_left = [(j, b) for j in range(B_TILES) for b in range(HID // BANK)]

        def less_bias(count):
            for n in range(min(count, len(less_bias_left))):
                j, b = less_bias_left.pop(0)
                cols = slice(BANK * b, BANK * (b + 1))
                nc.vector.tensor_tensor(
                    out=h_less_bias[:, j, cols], in0=h_sb[:, j, cols], in1=bias_all[:, cols], op=ALU.subtract
                )

        ct_codes = keep.tile([P, PASSES, BATCH], U32, align_bytes=256)
        ct_scales = keep.tile([P, PASSES, BATCH], U8, align_bytes=256)

        def transpose_halves(passes, half):
            pool, tag = (acc_psum, "acc") if half == 0 and 1 in passes else (flip_psum, "flip")
            banks = {g: pool.tile([P, 2, 2 * P], F32, tag=tag, name="flip") for g in passes}
            for jj in range(2):
                j = 2 * half + jj
                for g in passes:
                    if g == 0:
                        words = x_sb[:, j, :].bitcast(F32)
                    else:
                        words = h_sb[:, j, K_PASS * (g - 1) : K_PASS * g].bitcast(F32)
                    for u in range(2):
                        nc.tensor.transpose(
                            banks[g][:, u, P * jj : P * (jj + 1)], words[:, u : 2 * P : 2], ident_f32[:]
                        )
            return banks

        def regroup(bank, half, grouped, engine):
            source = bank[:].rearrange("p u b -> p b u")
            target = grouped[:].bitcast(F32).rearrange("p (b u) -> p b u", u=2)[:, 2 * P * half : 2 * P * (half + 1), :]
            if engine == "vector":
                nc.vector.tensor_copy(out=target, in_=source)
            else:
                nc.scalar.copy(out=target, in_=source)

        def quantise_pass(g, grouped):
            nc.vector.quantize_mx(out=ct_codes[:, g, :].bitcast(FP8X4), scales=ct_scales[:, g, :], in_=grouped[:])

        def weight_scale(planes, last, g, cols):
            if g < PLANES_PER_TILE:
                return planes[4 * g : P, cols]
            part = cols.start // LAST_COLS
            return last[4 * part : P, cols.start - LAST_COLS * part : cols.stop - LAST_COLS * part]

        def f_pass(acc, i, g):
            cols = slice(P * i, P * (i + 1))
            nc.tensor.matmul_mx(
                out=acc[:],
                lhsT=w_mod_sb[:, g, cols].bitcast(FP8X4),
                lhsT_scale=weight_scale(planes_mod, last_mod, g, cols),
                rhs=ct_codes[:, g, :].bitcast(FP8X4),
                rhs_scale=ct_scales[:, g, :],
                start=(g == 0),
                stop=(g == PASSES - 1),
            )

        def a_pass(acc, cols, j, g):
            rows = slice(P * j, P * (j + 1))
            nc.tensor.matmul_mx(
                out=acc,
                lhsT=ct_codes[:, g, rows].bitcast(FP8X4),
                lhsT_scale=ct_scales[:, g, rows],
                rhs=w_tgt_sb[:, g, cols].bitcast(FP8X4),
                rhs_scale=weight_scale(planes_tgt, last_tgt, g, cols),
                start=(g == 0),
                stop=(g == PASSES - 1),
            )

        inv_tau = keep.tile([P, U_TILES], F32)
        seed = keep.tile([P, U_TILES], F32)
        slope = keep.tile([P, U_TILES], F32)
        base = keep.tile([P, U_TILES], F32)
        neg_dt = keep.tile([P, B_TILES], F32)
        unit_cols = keep.tile([P, 2 * U_TILES], F32)
        b_mod_cols = unit_cols[:, 0:U_TILES]

        def unit_columns():
            unit_ps = flip_psum.tile([P, 2 * U_TILES], F32, tag="flip")
            nc.tensor.matmul(unit_ps[:], lhsT=unit_rows[:], rhs=ident_bf16[:, 0 : 2 * U_TILES], start=True, stop=True)
            return unit_ps

        def unit_constants():
            nc.scalar.activation(out=inv_tau[:], in_=unit_cols[:, U_TILES : 2 * U_TILES], func=ACT.Exp, scale=-1.0)
            nc.vector.tensor_scalar(out=neg_dt[:], in0=dt_sb[:], scalar1=-1.0, scalar2=None, op0=ALU.mult)
            nc.vector.tensor_scalar(out=seed[:], in0=inv_tau[:], scalar1=EPS, scalar2=1.0, op0=ALU.mult, op1=ALU.add)
            nc.vector.reciprocal(out=seed[:], in_=seed[:])
            nc.vector.tensor_tensor(out=slope[:], in0=seed[:], in1=seed[:], op=ALU.mult)
            nc.vector.tensor_tensor(out=base[:], in0=seed[:], in1=inv_tau[:], op=ALU.mult)
            nc.vector.scalar_tensor_tensor(
                out=base[:], in0=slope[:], scalar=-EPS, in1=base[:], op0=ALU.mult, op1=ALU.add
            )

        with tc.tile_pool(name="stage", bufs=1) as stage:
            grouped = []
            for g in range(PASSES):
                grouped.append(stage.tile([P, BATCH * PACK], BF16, align_bytes=256, tag="grouped%d" % g, name="grouped"))
            spread(bias_rows, bias_all)
            for half in range(2):
                regroup(transpose_halves([0], half)[0], half, grouped[0], "vector" if half else "scalar")
            spread(b_tgt_rows, b_tgt_all)
            quantise_pass(0, grouped[0])
            h_passes = list(range(1, PASSES))
            banks = transpose_halves(h_passes, 0)
            less_bias(6)
            unit_ps = unit_columns()
            for g in h_passes:
                regroup(banks[g], 0, grouped[g], "scalar")
                if g == 2:
                    nc.scalar.copy(out=unit_cols[:], in_=unit_ps[:])
            banks = transpose_halves(h_passes, 1)
            for g in h_passes:
                regroup(banks[g], 1, grouped[g], "scalar" if g > 1 else "vector")
                quantise_pass(g, grouped[g])
        unit_constants()
        work = ctx.enter_context(tc.tile_pool(name="work", bufs=4))

        tiles = [(r, j) for r in range(len(ROUNDS)) for j in range(B_TILES)]
        goal, decay, rates, abs_v, flips = {}, {}, {}, {}, {}

        def units(r):
            first, width = ROUNDS[r]
            return slice(first, first + width)

        def add_b_tgt(n, acc):
            r, j = tiles[n]
            goal[n] = work.tile([P, ROUNDS[r][1]], F32, tag="goal", bufs=8, name="goal")
            nc.vector.tensor_tensor(out=goal[n][:], in0=acc, in1=b_tgt_all[:, units(r)], op=ALU.add)

        def tanh_goal(n):
            nc.scalar.activation(out=goal[n][:], in_=goal[n][:], func=ACT.Tanh)

        def pull(n):
            r, j = tiles[n]
            nc.vector.tensor_tensor(
                out=goal[n][:], in0=goal[n][:], in1=h_less_bias[:, j, units(r)], op=ALU.subtract
            )

        def decay_of(n):
            r, j = tiles[n]
            decay[n] = work.tile([P, ROUNDS[r][1]], F32, tag="decay", bufs=6, name="decay")
            nc.scalar.activation(out=decay[n][:], in_=flips[n][:], func=ACT.Exp, scale=neg_dt[:, j : j + 1])

        def shrink(n):
            nc.vector.scalar_tensor_tensor(
                out=goal[n][:], in0=decay[n][:], scalar=-1.0, in1=goal[n][:], op0=ALU.add, op1=ALU.mult
            )

        def finish(n):
            r, j = tiles[n]
            new_h = work.tile([P, ROUNDS[r][1]], F32, tag="new_h", bufs=4, name="new_h")
            nc.vector.tensor_tensor(out=new_h[:], in0=h_sb[:, j, units(r)], in1=goal[n][:], op=ALU.subtract)
            nc.sync.dma_start(out=out_view[:, j, units(r)], in_=new_h[:])

        def abs_of(i, acc):
            abs_v[i] = work.tile([P, BATCH], F32, tag="abs_v", bufs=5, name="abs_v")
            nc.scalar.activation(out=abs_v[i][:], in_=acc[:], func=ACT.Abs, bias=b_mod_cols[:, i : i + 1])

        def tanh_f(i):
            nc.scalar.activation(out=abs_v[i][:], in_=abs_v[i][:], func=ACT.Tanh, bias=EPS)

        def rate_of(i):
            rates[i] = work.tile([P, BATCH], F32, tag="rate", bufs=6, name="rate")
            if i < VECTOR_RATES:
                nc.vector.tensor_scalar(
                    out=rates[i][:], in0=abs_v[i][:], scalar1=slope[:, i : i + 1], scalar2=base[:, i : i + 1],
                    op0=ALU.mult, op1=ALU.add,
                )
            else:
                nc.scalar.activation(
                    out=rates[i][:], in_=abs_v[i][:], func=ACT.Identity, scale=slope[:, i : i + 1], bias=base[:, i : i + 1]
                )

        def flip_rates(r):
            first, width = ROUNDS[r]
            for j in range(B_TILES):
                flip = flip_psum.tile([P, width], F32, tag="flip", name="flip")
                for ii in range(width // P):
                    nc.tensor.transpose(
                        flip[:, P * ii : P * (ii + 1)], rates[first // P + ii][:, P * j : P * (j + 1)], ident_f32[:]
                    )
                flips[B_TILES * r + j] = flip

        def f_group(i):
            acc = acc_psum.tile([P, BATCH], F32, tag="acc", name="acc")
            for g in range(PASSES):
                f_pass(acc, i, g)
            return acc

        def a_group(n):
            r, j = tiles[n]
            pool, tag = (flip_psum, "flip") if n < 2 else (acc_psum, "acc")
            acc = pool.tile([P, BANK], F32, tag=tag, name="acc")
            part = acc[:, 0 : ROUNDS[r][1]]
            for g in range(PASSES):
                a_pass(part, units(r), j, g)
            return part

        accs = [acc_psum.tile([P, BATCH], F32, tag="acc", name="acc") for i in range(HEAD_TILES)]
        for g in range(PASSES):
            for i in range(HEAD_TILES):
                f_pass(accs[i], i, g)
        less_bias(10)
        for i in range(HEAD_TILES):
            abs_of(i, accs[i])

        f_after = {2: [4, 5], 3: [6, 7], 4: [8], 5: [9], 6: [10], 7: [11], 8: [12], 10: [13], 11: [14], 13: [15]}
        flip_after = {2: 0, 5: 1, 9: 2, 13: 3, 17: 4}
        f_waiting = list(range(HEAD_TILES))
        to_decay, decayed = [], []
        late_loads = {4: (W_mod_words, w_mod_sb, 1536), 6: (W_tgt_words, w_tgt_sb, 1536)}
        for n in range(len(tiles)):
            acc = a_group(n)
            for i in f_waiting:
                tanh_f(i)
            for m in to_decay[0:2]:
                decay_of(m)
            decayed += to_decay[0:2]
            to_decay = to_decay[2:]
            for i in f_waiting:
                if i >= VECTOR_RATES:
                    rate_of(i)
            add_b_tgt(n, acc)
            tanh_goal(n)
            for i in f_waiting:
                if i < VECTOR_RATES:
                    rate_of(i)
            blends = [m for m in decayed[0:2] if m < n - 1]
            decayed = decayed[len(blends) :]
            for m in blends:
                shrink(m)
            if n > 0:
                pull(n - 1)
            for m in blends:
                finish(m)
            less_bias(1)
            if n in late_loads:
                load_words(*late_loads[n], slice(0, 5))
            f_waiting = []
            for i in f_after.get(n, []):
                abs_of(i, f_group(i))
                f_waiting.append(i)
            if n in flip_after:
                r = flip_after[n]
                flip_rates(r)
                to_decay = to_decay + list(range(B_TILES * r, B_TILES * (r + 1)))
        pull(len(tiles) - 1)
        for m in to_decay:
            decay_of(m)
        for m in decayed + to_decay:
            shrink(m)
        for m in decayed + to_decay:
            finish(m)
